import numpy as np
import ml_dtypes


def mxq(x, axis, fmt="e4m3"):
    dtype, down = {"e4m3": (ml_dtypes.float8_e4m3fn, 7), "e5m2": (ml_dtypes.float8_e5m2, 14)}[fmt]
    v = np.moveaxis(np.asarray(x, np.float32).astype(ml_dtypes.bfloat16).astype(np.float64), axis, -1)
    blocks = v.reshape(v.shape[:-1] + (-1, 32))
    amax = np.abs(blocks).max(-1, keepdims=True)
    byte = np.maximum(np.where(amax > 0, np.frexp(amax)[1] - 1 + 127, 0) - down, 1)
    scale = np.exp2(byte - 127.0)
    codes = (blocks / scale).astype(np.float32).astype(dtype).astype(np.float64)
    return np.moveaxis((codes * scale).reshape(v.shape), -1, axis)


WIDE = False


def mx_kscale(k):
    if not WIDE:
        return np.ones(k)
    levels = np.array([10, -10, 5, -5, 0])
    a = np.random.permutation(np.resize(levels, k // 512 * 4)).reshape(k // 512, 4)
    idx = np.arange(k)
    return np.exp2(a[idx // 512, idx % 128 // 32])


BF16 = ml_dtypes.bfloat16


def bf(x):
    return np.asarray(x, np.float32).astype(BF16)


def f64(x):
    return np.asarray(x).astype(np.float64)


BATCH, IN_FEATURES, OUT_FEATURES = 4096, 32, 1024
DEGREE = IN_FEATURES - 1


def _bspline_basis(x, degree, knots):
    xe = x[..., None]
    nk = knots.shape[0]
    bas = np.where((knots[:-1] <= xe) & (xe < knots[1:]), 1.0, 0.0)
    for k in range(1, degree + 1):
        n = nk - k - 1
        d1 = knots[k:k + n] - knots[:n]
        d2 = knots[k + 1:k + 1 + n] - knots[1:n + 1]
        w1 = np.where(d1 != 0, (xe - knots[:n]) / np.where(d1 != 0, d1, 1.0), 0.0)
        w2 = np.where(d2 != 0, (knots[k + 1:k + 1 + n] - xe) / np.where(d2 != 0, d2, 1.0), 0.0)
        bas = w1 * bas[..., :n] + w2 * bas[..., 1:n + 1]
    return bas


def setup_inputs():
    s = np.asarray(mx_kscale(IN_FEATURES * (DEGREE + 1)), np.float64)[::DEGREE + 1]
    r = s / s.min()
    e = np.log2(r)
    knots = np.linspace(-1.0, 1.0, DEGREE + IN_FEATURES + 1)
    grid = np.linspace(0.2, 1.6, 2801)
    drop = np.maximum.accumulate(-np.log2(_bspline_basis(np.tanh(grid)[:, None], DEGREE, knots).sum(axis=(1, 2))))
    z = np.random.standard_normal((BATCH, IN_FEATURES))
    sg = np.where(np.random.standard_normal((BATCH, IN_FEATURES)) < 0.0, -1.0, 1.0)
    far = sg * np.interp(e + 2.0 + z, drop, grid)
    x = np.where(e > 0, far, z)
    coef = np.random.standard_normal((IN_FEATURES, OUT_FEATURES, DEGREE + 1)) * 1.6 / IN_FEATURES ** 0.25 * r[:, None, None]
    return {"x": bf(x), "coefficients": bf(coef)}


def reference(x, coefficients):
    t = np.tanh(f64(x))
    knots = np.linspace(-1.0, 1.0, DEGREE + IN_FEATURES + 1)
    basis = _bspline_basis(t, DEGREE, knots)
    a = basis.reshape(BATCH, IN_FEATURES * (DEGREE + 1))
    w = f64(coefficients).transpose(0, 2, 1).reshape(IN_FEATURES * (DEGREE + 1), OUT_FEATURES)
    return mxq(a, 1, "e4m3") @ mxq(w, 0, "e4m3")

@@ -1,0 +1,502 @@
+from contextlib import ExitStack
+
+import concourse.mybir as mybir
+from concourse.masks import make_identity
+
+FLOPS = 2 * 4096 * 1024 * 1024
+
+F32 = mybir.dt.float32
+BF16 = mybir.dt.bfloat16
+I32 = mybir.dt.int32
+U32 = mybir.dt.uint32
+U8 = mybir.dt.uint8
+FP8X4 = mybir.dt.float8_e4m3fn_x4
+ACT = mybir.ActivationFunctionType
+ALU = mybir.AluOpType
+AX = mybir.AxisListType
+
+P = 128
+NB = 4096
+NI = 32
+NO = 1024
+NT = NB // P
+NP = NT * NI
+ND = NT // 2
+W2 = 2 * NI
+ROWS = 80
+UMAX = 62.99999
+
+
+def binomial(n, k):
+    v = 1
+    for j in range(k):
+        v = v * (n - j) // (j + 1)
+    return v
+
+
+def factorial31():
+    v = 1
+    for j in range(2, 32):
+        v = v * j
+    return v
+
+
+def taylor_coefficient(r, p):
+    total = 0
+    for k in range(r + 1):
+        total += (-1) ** k * binomial(32, k) * (2 * (r - k) + 1) ** (31 - p)
+    return float(binomial(31, p) * total) / float(factorial31() * 2 ** (31 - p))
+
+
+def to_float32(v):
+    if v == 0.0:
+        return 0.0
+    s = abs(v)
+    e = 0
+    while s >= 2.0:
+        s = s / 2.0
+        e += 1
+    while s < 1.0:
+        s = s * 2.0
+        e -= 1
+    m = float(round(s * 8388608.0)) * 2.0 ** (e - 23)
+    return m if v > 0.0 else -m
+
+
+def mirror_rows(m):
+    return slice(m, 8 - m, 7 - 2 * m)
+
+
+def chi(k, e):
+    return 1 if ((e >> k) & 1) == 0 else -1
+
+
+def row_groups(lo, hi, sign_of, want):
+    runs = []
+    e = lo
+    while e < hi:
+        if sign_of(e) == want:
+            s = e
+            while e < hi and sign_of(e) == want:
+                e += 1
+            runs.append((s, e - s))
+        else:
+            e += 1
+    groups = []
+    n = 0
+    while n < len(runs):
+        s, ln = runs[n]
+        cnt = 1
+        per = 0
+        while n + cnt < len(runs) and runs[n + cnt][1] == ln:
+            step = runs[n + cnt][0] - runs[n + cnt - 1][0]
+            if cnt == 1:
+                per = step
+            if step != per:
+                break
+            cnt += 1
+        if cnt == 1:
+            per = 0
+        groups.append((s, ln, cnt, per))
+        n += cnt
+    return groups
+
+
+def rows_view(buf, grp, shift):
+    s, ln, cnt, per = grp
+    s = s - shift
+    if cnt == 1:
+        return buf[:, s : s + ln, :]
+    return buf[:, s : s + cnt * per, :].rearrange("q (z r) w -> q z r w", r=per)[:, :, 0:ln, :]
+
+
+def pair_rows(arr, p0, grp):
+    s, ln, cnt, per = grp
+    v = arr[:, p0 : p0 + W2].unsqueeze(1)
+    if cnt == 1:
+        return v.to_broadcast([P, ln, W2])
+    return v.unsqueeze(1).to_broadcast([P, cnt, ln, W2])
+
+
+def tile_kanlinear_t_kernel(tc, x, coefficients, out):
+    nc = tc.nc
+    c31 = pow(float(factorial31()), -1.0 / 31.0)
+    out_v = out.rearrange("(p t) o -> t p o", t=NT)
+    coef_v = coefficients.rearrange("i (a o) d -> a o i d", o=P)
+
+    with ExitStack() as ctx:
+        ctx.enter_context(tc.manual_schedule())
+        keep = ctx.enter_context(tc.tile_pool(name="keep", bufs=1))
+        psum = ctx.enter_context(tc.psum_pool(name="psum", bufs=2))
+        work = ctx.enter_context(tc.tile_pool(name="work", bufs=2))
+        wp = ctx.enter_context(tc.tile_pool(name="wp", bufs=2))
+
+        ident_f = keep.tile([P, P], F32)
+        make_identity(nc, ident_f[:])
+        ident_b = keep.tile([P, P], BF16)
+        make_identity(nc, ident_b[:])
+
+        wmat = keep.tile([P, 24, 4], F32)
+        w_codes = keep.tile([P, 2, NO], U32, align_bytes=64)
+        w_scales = keep.tile([P, 2, NO], U8, align_bytes=64)
+        hh = keep.tile([P, NP], F32)
+        mu_pos = []
+        mu_neg = []
+        for k in range(5):
+            mu_pos.append(keep.tile([P, NP], BF16, name="mu_pos%d" % k))
+            mu_neg.append(keep.tile([P, NP], BF16, name="mu_neg%d" % k))
+        ml_pos = keep.tile([P, NP], BF16)
+        ml_neg = keep.tile([P, NP], BF16)
+        mr_pos = keep.tile([P, NP], BF16)
+        mr_neg = keep.tile([P, NP], BF16)
+        xe = keep.tile([P, 8, NP], BF16)
+
+        tb_hi = keep.tile([P, 12, 2, 16], F32)
+        tb_lo = keep.tile([P, 12, 2, 8], F32)
+        for s in range(16):
+            for odd in range(2):
+                for r in range(4, 16):
+                    v = taylor_coefficient(r, 2 * s + odd)
+                    hi = to_float32(v)
+                    nc.gpsimd.memset(tb_hi[:, r - 4, odd, s : s + 1], hi)
+                    if s < 8:
+                        nc.gpsimd.memset(tb_lo[:, r - 4, odd, s : s + 1], to_float32(v - hi))
+
+        with tc.tile_pool(name="pre", bufs=1) as pre:
+            xb = pre.tile([P, NP], BF16)
+            nc.sync.dma_start(out=xb[:], in_=x.rearrange("(p t) i -> p (t i)", t=NT))
+            th = pre.tile([P, NP], F32, tag="rot", bufs=3)
+            nc.scalar.activation(out=th[:], in_=xb[:], func=ACT.Tanh)
+
+            gw = wp.tile([P, 2, NO, 4], BF16, align_bytes=64, bufs=1)
+            for a in range(8):
+                cw = wp.tile([P, NI, 32], BF16)
+                nc.sync.dma_start(out=cw[:], in_=coef_v[a])
+                cw2 = wp.tile([P, 4, NI, 8], BF16)
+                nc.scalar.copy(out=cw2[:], in_=cw[:].rearrange("q i (t s) -> q t i s", s=8))
+                wt = psum.tile([P, 2, 4, P], BF16, tag="xt")
+                for c in range(2):
+                    for tq in range(4):
+                        nc.tensor.transpose(
+                            out=wt[:, c, tq, :],
+                            in_=cw2[:, tq, c * 16 : (c + 1) * 16, :].rearrange("q i s -> q (i s)"),
+                            identity=ident_b[:],
+                        )
+                nc.scalar.copy(out=gw[:, :, a * P : (a + 1) * P, :], in_=wt[:].rearrange("q c t r -> q c r t"))
+
+            u0 = pre.tile([P, NP], F32, tag="rot", bufs=3)
+            nc.vector.tensor_scalar(out=u0[:], in0=th[:], scalar1=31.5, scalar2=31.5, op0=ALU.mult, op1=ALU.add)
+            uu = pre.tile([P, NP], F32)
+            nc.vector.tensor_scalar(out=uu[:], in0=u0[:], scalar1=UMAX, scalar2=0.0, op0=ALU.min, op1=ALU.max)
+            ji = pre.tile([P, NP], I32)
+            nc.vector.tensor_copy(out=ji[:], in_=uu[:])
+            jf = pre.tile([P, NP], F32, tag="rot", bufs=3)
+            nc.vector.tensor_copy(out=jf[:], in_=ji[:])
+            fr = pre.tile([P, NP], F32, tag="rot", bufs=3)
+            nc.vector.tensor_tensor(out=fr[:], in0=uu[:], in1=jf[:], op=ALU.subtract)
+            j1a = pre.tile([P, NP], F32, tag="rot", bufs=3)
+            nc.vector.scalar_tensor_tensor(out=j1a[:], in0=fr[:], scalar=1.0, in1=jf[:], op0=ALU.is_ge, op1=ALU.add)
+            j1b = pre.tile([P, NP], F32, tag="rot", bufs=3)
+            nc.vector.scalar_tensor_tensor(out=j1b[:], in0=fr[:], scalar=0.0, in1=j1a[:], op0=ALU.is_ge, op1=ALU.add)
+            j1i = pre.tile([P, NP], I32)
+            nc.vector.tensor_copy(out=j1i[:], in_=j1b[:])
+            j1 = pre.tile([P, NP], F32, tag="rot", bufs=3)
+            nc.vector.tensor_copy(out=j1[:], in_=j1i[:])
+            hm = pre.tile([P, NP], F32, tag="rot", bufs=3)
+            nc.vector.tensor_tensor(out=hm[:], in0=uu[:], in1=j1[:], op=ALU.subtract)
+            nc.vector.tensor_scalar_add(out=hh[:], in0=hm[:], scalar1=0.5)
+
+            bit5 = pre.tile([P, NP], I32, tag="bit", bufs=2)
+            nc.vector.tensor_scalar(out=bit5[:], in0=j1i[:], scalar1=5, scalar2=1, op0=ALU.logical_shift_right, op1=ALU.bitwise_and)
+            b5 = pre.tile([P, NP], BF16)
+            nc.vector.tensor_copy(out=b5[:], in_=bit5[:])
+            for k in (4, 3, 2, 1, 0):
+                bit = pre.tile([P, NP], I32, tag="bit", bufs=2)
+                nc.vector.tensor_scalar(out=bit[:], in0=j1i[:], scalar1=k, scalar2=1, op0=ALU.logical_shift_right, op1=ALU.bitwise_and)
+                nc.vector.tensor_scalar(out=mu_pos[k][:], in0=bit[:], scalar1=-2.0, scalar2=1.0, op0=ALU.mult, op1=ALU.add)
+                nc.vector.tensor_scalar(out=mu_neg[k][:], in0=bit[:], scalar1=2.0, scalar2=-1.0, op0=ALU.mult, op1=ALU.add)
+            nc.vector.tensor_tensor(out=mr_pos[:], in0=mu_pos[4][:], in1=b5[:], op=ALU.mult)
+            nc.vector.tensor_tensor(out=ml_pos[:], in0=mu_pos[4][:], in1=mr_pos[:], op=ALU.subtract)
+            nc.vector.tensor_scalar_mul(out=mr_neg[:], in0=mr_pos[:], scalar1=-1.0)
+            nc.vector.tensor_scalar_mul(out=ml_neg[:], in0=ml_pos[:], scalar1=-1.0)
+
+        def pair_view(arr, p0):
+            return arr[:, p0 : p0 + W2].rearrange("q (c g) -> q c g", g=4)
+
+        def taylor_matrix():
+            lo_part = tb_hi[:, :, :, 0:8]
+            nc.vector.tensor_tensor(out=lo_part, in0=lo_part, in1=tb_lo[:], op=ALU.add)
+            dmask = wp.tile([P, 32], F32, bufs=1)
+            nc.vector.tensor_reduce(out=dmask[:], in_=ident_f[:].rearrange("q (p g) -> q p g", g=4), axis=AX.X, op=ALU.add)
+            gmask = wp.tile([P, 4], F32, bufs=1)
+            nc.vector.tensor_reduce(out=gmask[:], in_=ident_f[:].rearrange("q (p g) -> q g p", g=4), axis=AX.X, op=ALU.add)
+            alt = wp.tile([P, 32], F32, bufs=1)
+            nc.vector.memset(alt[:, 0:16], 1.0)
+            nc.vector.memset(alt[:, 16:32], -1.0)
+            sa = wp.tile([P, 32], F32, bufs=1)
+            nc.vector.tensor_tensor(out=sa[:], in0=dmask[:], in1=alt[:], op=ALU.mult)
+            sgnp = wp.tile([P, 1], F32, bufs=1)
+            nc.vector.tensor_reduce(out=sgnp[:], in_=sa[:], axis=AX.X, op=ALU.add)
+            t1 = wp.tile([P, 12, 32], F32, bufs=1)
+            nc.vector.tensor_tensor(
+                out=t1[:],
+                in0=tb_hi[:].rearrange("q r h s -> q r (h s)"),
+                in1=dmask[:].unsqueeze(1).to_broadcast([P, 12, 32]),
+                op=ALU.mult,
+            )
+            w0 = wp.tile([P, 12], F32, bufs=1)
+            nc.vector.tensor_reduce(out=w0[:], in_=t1[:], axis=AX.X, op=ALU.add)
+            wc = wp.tile([P, 24], F32, bufs=1)
+            nc.vector.tensor_scalar(out=wc[:, 0:12], in0=w0[:], scalar1=sgnp[:, 0:1], scalar2=None, op0=ALU.mult)
+            for e in range(16, 28):
+                nc.vector.tensor_copy(out=wc[:, e - 4 : e - 3], in_=w0[:, 27 - e : 28 - e])
+            nc.vector.tensor_tensor(
+                out=wmat[:],
+                in0=wc[:].unsqueeze(2).to_broadcast([P, 24, 4]),
+                in1=gmask[:].unsqueeze(1).to_broadcast([P, 24, 4]),
+                op=ALU.mult,
+            )
+
+        def quantise_weights():
+            for c in range(2):
+                nc.vector.quantize_mx(
+                    out=w_codes[:, c, :].bitcast(FP8X4),
+                    scales=w_scales[:, c, :],
+                    in_=gw[:, c, :, :].rearrange("q o t -> q (o t)"),
+                )
+
+        def powers_scalar(ph, duo, level):
+            hv = pair_view(hh, duo * W2)
+            if level == 0:
+                nc.scalar.activation(out=ph[:, :, 0, :], in_=hv, func=ACT.Identity, scale=0.0, bias=1.0)
+                nc.scalar.activation(out=ph[:, :, 1, :], in_=hv, func=ACT.Square)
+            else:
+                n = 1 << (level - 1)
+                nc.scalar.activation(out=ph[:, :, 2 * n : 4 * n : 2, :], in_=ph[:, :, n : 2 * n, :], func=ACT.Square)
+                nc.scalar.activation(out=ph[:, :, 2 * n + 1 : 4 * n : 2, :], in_=ph[:, :, 16 + n : 16 + 2 * n, :], func=ACT.Square)
+
+        def powers_vector(ph, duo, level):
+            lo = 0 if level == 0 else 1 << level
+            hi = 2 << level
+            nc.vector.tensor_tensor(
+                out=ph[:, :, 16 + lo : 16 + hi, :],
+                in0=ph[:, :, lo:hi, :],
+                in1=pair_view(hh, duo * W2).unsqueeze(2).to_broadcast([P, 16, hi - lo, 4]),
+                op=ALU.mult,
+            )
+
+        def pieces_a(ph, q):
+            ft = psum.tile([P, 4, P], F32, tag="ft")
+            for s in range(4):
+                nc.tensor.transpose(out=ft[:, s, :], in_=ph[:, q * 4 + s, :, :].rearrange("q p g -> q (p g)"), identity=ident_f[:])
+            fts = work.tile([P, 4, P], F32, tag="fts")
+            nc.scalar.copy(out=fts[:], in_=ft[:])
+            return fts
+
+        def pieces_b(fts):
+            pa = psum.tile([P, 512], F32, tag="pa")
+            for s in range(4):
+                nc.tensor.matmul(out=pa[:, s * 96 : (s + 1) * 96], lhsT=fts[:, s, :], rhs=wmat[:].rearrange("q e g -> q (e g)"), start=True, stop=True)
+            return pa
+
+        def pieces_c(at, pa, q):
+            nc.scalar.copy(
+                out=at[:, 4:28, q * 16 : (q + 1) * 16].rearrange("q e (s g) -> q e s g", g=4),
+                in_=pa[:, 0:384].rearrange("q (s e g) -> q e s g", s=4, e=24, g=4),
+            )
+
+        def pieces_outer(at, duo):
+            nc.scalar.copy(out=at[:, 0:4, :], in_=xe[:, 0:4, duo * W2 : (duo + 1) * W2])
+            nc.scalar.copy(out=at[:, 28:32, :], in_=xe[:, 4:8, duo * W2 : (duo + 1) * W2])
+
+        def shift_stage(duo, k, src):
+            p0 = duo * W2
+            a = 1 << k
+            out_lo = 32 - a if k > 0 else 32
+            gcur = work.tile([P, ROWS, W2], BF16, tag="gs")
+            if k == 4:
+                for off, m_pos, m_neg in ((0, ml_pos, ml_neg), (32, mr_pos, mr_neg)):
+                    for row, mm in ((0, m_pos), (16, m_neg)):
+                        grp = (off + row, 16, 1, 0)
+                        nc.vector.tensor_tensor(out=rows_view(gcur, grp, 0), in0=src[:, row : row + 16, :], in1=pair_rows(mm, p0, grp), op=ALU.mult)
+            else:
+                for want, mu in ((1, mu_pos[k]), (-1, mu_neg[k])):
+                    for grp in row_groups(out_lo - a, 64, lambda e: chi(k + 1, e) * chi(k, e), want):
+                        nc.vector.tensor_tensor(out=rows_view(gcur, grp, 0), in0=rows_view(src, grp, 0), in1=pair_rows(mu, p0, grp), op=ALU.mult)
+            if k > 0:
+                ycur = work.tile([P, ROWS, W2], BF16, tag="ys")
+                base = 0
+            else:
+                ycur = work.tile([P, 34, W2], BF16, tag="yfin")
+                base = 32
+            for want, op in ((1, ALU.max), (-1, ALU.min)):
+                for grp in row_groups(out_lo, 64, lambda e: chi(k, e), want):
+                    nc.vector.tensor_tensor(out=rows_view(ycur, grp, base), in0=rows_view(gcur, grp, 0), in1=rows_view(gcur, grp, a), op=op)
+            return ycur
+
+        def turn_a(yfin, a):
+            yc = work.tile([P, 4, NI, 8], BF16, tag="yc")
+            nc.scalar.activation(out=yc[:], in_=yfin[:, 0:32, a * NI : (a + 1) * NI].rearrange("q (t s) i -> q t i s", s=8), func=ACT.Abs)
+            return yc
+
+        def turn_b(yc):
+            xt = psum.tile([P, 2, 4, P], BF16, tag="xt")
+            for c in range(2):
+                for tq in range(4):
+                    nc.tensor.transpose(out=xt[:, c, tq, :], in_=yc[:, tq, c * 16 : (c + 1) * 16, :].rearrange("q i s -> q (i s)"), identity=ident_b[:])
+            return xt
+
+        def turn_c(xt):
+            grouped = work.tile([P, 2, P, 4], BF16, tag="grouped", align_bytes=64)
+            nc.scalar.copy(out=grouped[:], in_=xt[:].rearrange("q c t r -> q c r t"))
+            return grouped
+
+        def multiply(t, grouped):
+            b_codes = work.tile([P, 2 * P], U32, tag="b_codes", align_bytes=64)
+            b_scales = work.tile([P, 2 * P], U8, tag="b_scales", align_bytes=64)
+            nc.vector.quantize_mx(out=b_codes[:].bitcast(FP8X4), scales=b_scales[:], in_=grouped[:].rearrange("q c r t -> q (c r t)"))
+            res = work.tile([P, NO], F32, tag="res", bufs=3)
+            for n in range(2):
+                acc = psum.tile([P, 512], F32, tag="acc")
+                for c in range(2):
+                    nc.tensor.matmul_mx(
+                        out=acc[:],
+                        lhsT=b_codes[:, c * P : (c + 1) * P].bitcast(FP8X4),
+                        lhsT_scale=b_scales[:, c * P : (c + 1) * P],
+                        rhs=w_codes[:, c, n * 512 : (n + 1) * 512].bitcast(FP8X4),
+                        rhs_scale=w_scales[:, c, n * 512 : (n + 1) * 512],
+                        start=(c == 0),
+                        stop=(c == 1),
+                    )
+                nc.scalar.copy(out=res[:, n * 512 : (n + 1) * 512], in_=acc[:])
+            nc.sync.dma_start(out=out_v[t], in_=res[:])
+
+        ph_of = {}
+        for duo in range(2):
+            ph_new = work.tile([P, 16, 32, 4], F32, tag="ph")
+            ph_of[duo] = ph_new
+            for level in range(4):
+                powers_scalar(ph_new, duo, level)
+                powers_vector(ph_new, duo, level)
+
+        with tc.tile_pool(name="ex", bufs=2) as ex:
+            cn = 64
+            nch = NP // cn
+            qq_of = {}
+            for ch in range(nch + 1):
+                if ch < nch:
+                    c0 = ch * cn
+                    xs1 = ex.tile([P, 8, cn], F32, tag="xs1")
+                    for m in range(4):
+                        nc.scalar.activation(out=xs1[:, m, :], in_=hh[:, c0 : c0 + cn], func=ACT.Identity, scale=-c31, bias=c31 * (m + 0.5))
+                        nc.scalar.activation(out=xs1[:, 7 - m, :], in_=hh[:, c0 : c0 + cn], func=ACT.Identity, scale=c31, bias=c31 * (m + 0.5))
+                    xs2 = ex.tile([P, 8, cn], F32, tag="xs2")
+                    nc.scalar.activation(out=xs2[:], in_=xs1[:], func=ACT.Square)
+                    xs4 = ex.tile([P, 8, cn], F32, tag="xs4")
+                    nc.scalar.activation(out=xs4[:], in_=xs2[:], func=ACT.Square)
+                    xs8 = ex.tile([P, 8, cn], F32, tag="xs8")
+                    nc.scalar.activation(out=xs8[:], in_=xs4[:], func=ACT.Square)
+                    xs16 = ex.tile([P, 8, cn], F32, tag="xs16")
+                    nc.scalar.activation(out=xs16[:], in_=xs8[:], func=ACT.Square)
+                if ch > 0:
+                    prev = (ch - 1) * cn
+                    nc.scalar.copy(out=xe[:, mirror_rows(0), prev : prev + cn], in_=qq_of[ch - 1][:, mirror_rows(0), :])
+                if ch < nch:
+                    pr1 = ex.tile([P, 8, cn], F32, tag="pr1")
+                    nc.vector.tensor_tensor(out=pr1[:], in0=xs1[:], in1=xs2[:], op=ALU.mult)
+                    pr2 = ex.tile([P, 8, cn], F32, tag="pr2")
+                    nc.vector.tensor_tensor(out=pr2[:], in0=xs4[:], in1=xs8[:], op=ALU.mult)
+                    pr3 = ex.tile([P, 8, cn], F32, tag="pr3")
+                    nc.vector.tensor_tensor(out=pr3[:], in0=pr1[:], in1=pr2[:], op=ALU.mult)
+                    qq = ex.tile([P, 8, cn], F32, tag="qq")
+                    qq_of[ch] = qq
+                    nc.vector.tensor_tensor(out=qq[:], in0=pr3[:], in1=xs16[:], op=ALU.mult)
+                    xec = xe[:, :, c0 : c0 + cn]
+                    nc.vector.scalar_tensor_tensor(out=xec[:, mirror_rows(1), :], in0=qq[:, mirror_rows(0), :], scalar=-32.0, in1=qq[:, mirror_rows(1), :], op0=ALU.mult, op1=ALU.add)
+                    ta = ex.tile([P, 2, cn], F32, tag="ta")
+                    nc.vector.scalar_tensor_tensor(out=ta[:], in0=qq[:, mirror_rows(1), :], scalar=-32.0, in1=qq[:, mirror_rows(2), :], op0=ALU.mult, op1=ALU.add)
+                    nc.vector.scalar_tensor_tensor(out=xec[:, mirror_rows(2), :], in0=qq[:, mirror_rows(0), :], scalar=496.0, in1=ta[:], op0=ALU.mult, op1=ALU.add)
+                    tb3 = ex.tile([P, 2, cn], F32, tag="tb3")
+                    nc.vector.scalar_tensor_tensor(out=tb3[:], in0=qq[:, mirror_rows(2), :], scalar=-32.0, in1=qq[:, mirror_rows(3), :], op0=ALU.mult, op1=ALU.add)
+                    tc3 = ex.tile([P, 2, cn], F32, tag="tc3")
+                    nc.vector.scalar_tensor_tensor(out=tc3[:], in0=qq[:, mirror_rows(1), :], scalar=496.0, in1=tb3[:], op0=ALU.mult, op1=ALU.add)
+                    nc.vector.scalar_tensor_tensor(out=xec[:, mirror_rows(3), :], in0=qq[:, mirror_rows(0), :], scalar=-4960.0, in1=tc3[:], op0=ALU.mult, op1=ALU.add)
+                if ch == 11:
+                    taylor_matrix()
+        quantise_weights()
+
+        at_cur = work.tile([P, 32, W2], BF16, tag="at")
+        for q in range(4):
+            fts = pieces_a(ph_of[0], q)
+            pa = pieces_b(fts)
+            pieces_c(at_cur, pa, q)
+        pieces_outer(at_cur, 0)
+
+        yfin_prev = None
+        for n in range(ND + 1):
+            shifting = n < ND
+            finishing = n >= 1
+            piecing = n + 1 < ND
+            powering = n + 2 < ND
+            if powering:
+                ph_new = work.tile([P, 16, 32, 4], F32, tag="ph")
+                ph_of[n + 2] = ph_new
+                powers_scalar(ph_new, n + 2, 0)
+            if finishing:
+                yc0 = turn_a(yfin_prev, 0)
+            if piecing:
+                at_next = work.tile([P, 32, W2], BF16, tag="at")
+                fts0 = pieces_a(ph_of[n + 1], 0)
+            if finishing:
+                xt0 = turn_b(yc0)
+            if piecing:
+                pa0 = pieces_b(fts0)
+            if finishing:
+                yc1 = turn_a(yfin_prev, 1)
+                grouped0 = turn_c(xt0)
+            if shifting:
+                ycur = shift_stage(n, 4, at_cur)
+            if powering:
+                powers_vector(ph_new, n + 2, 0)
+                powers_scalar(ph_new, n + 2, 1)
+            if piecing:
+                pieces_c(at_next, pa0, 0)
+                fts1 = pieces_a(ph_of[n + 1], 1)
+            if finishing:
+                xt1 = turn_b(yc1)
+            if piecing:
+                pa1 = pieces_b(fts1)
+            if finishing:
+                grouped1 = turn_c(xt1)
+            if piecing:
+                pieces_c(at_next, pa1, 1)
+            if shifting:
+                ycur = shift_stage(n, 3, ycur)
+            if powering:
+                powers_vector(ph_new, n + 2, 1)
+                powers_scalar(ph_new, n + 2, 2)
+            if piecing:
+                for q in (2, 3):
+                    fts = pieces_a(ph_of[n + 1], q)
+                    pa = pieces_b(fts)
+                    pieces_c(at_next, pa, q)
+            if shifting:
+                ycur = shift_stage(n, 2, ycur)
+            if powering:
+                powers_vector(ph_new, n + 2, 2)
+                powers_scalar(ph_new, n + 2, 3)
+            if piecing:
+                pieces_outer(at_next, n + 1)
+            if shifting:
+                ycur = shift_stage(n, 1, ycur)
+            if powering:
+                powers_vector(ph_new, n + 2, 3)
+            if shifting:
+                ycur = shift_stage(n, 0, ycur)
+            if finishing:
+                multiply(2 * (n - 1), grouped0)
+                multiply(2 * (n - 1) + 1, grouped1)
+            if shifting:
+                yfin_prev = ycur
+            if piecing:
+                at_cur = at_next

@@ -25,6 +25,7 @@ ND = NT // 2
 W2 = 2 * NI
 ROWS = 80
 UMAX = 62.99999
+NLO = 8
 
 
 def binomial(n, k):
@@ -151,16 +152,32 @@ def tile_kanlinear_t_kernel(tc, x, coefficients, out):
         mr_neg = keep.tile([P, NP], BF16)
         xe = keep.tile([P, 8, NP], BF16)
 
-        tb_hi = keep.tile([P, 12, 2, 16], F32)
-        tb_lo = keep.tile([P, 12, 2, 8], F32)
-        for s in range(16):
-            for odd in range(2):
-                for r in range(4, 16):
-                    v = taylor_coefficient(r, 2 * s + odd)
-                    hi = to_float32(v)
-                    nc.gpsimd.memset(tb_hi[:, r - 4, odd, s : s + 1], hi)
-                    if s < 8:
-                        nc.gpsimd.memset(tb_lo[:, r - 4, odd, s : s + 1], to_float32(v - hi))
+        tb_hi = keep.tile([P, 12, 32], F32)
+        tb_lo = keep.tile([P, 12, NLO], F32)
+        for p in range(32):
+            for r in range(4, 16):
+                v = taylor_coefficient(r, p)
+                hi = to_float32(v)
+                nc.gpsimd.memset(tb_hi[:, r - 4, p : p + 1], hi)
+                if p < NLO:
+                    nc.vector.memset(tb_lo[:, r - 4, p : p + 1], to_float32(v - hi))
+
+        gw = wp.tile([P, 2, NO, 4], BF16, align_bytes=64, bufs=1)
+
+        def weights_block(a):
+            cw = wp.tile([P, NI, 32], BF16, tag="cw")
+            nc.sync.dma_start(out=cw[:], in_=coef_v[a])
+            cw2 = wp.tile([P, 4, NI, 8], BF16, tag="cw2")
+            nc.scalar.copy(out=cw2[:], in_=cw[:].rearrange("q i (t s) -> q t i s", s=8))
+            wt = psum.tile([P, 2, 4, P], BF16, tag="xt")
+            for c in range(2):
+                for tq in range(4):
+                    nc.tensor.transpose(
+                        out=wt[:, c, tq, :],
+                        in_=cw2[:, tq, c * 16 : (c + 1) * 16, :].rearrange("q i s -> q (i s)"),
+                        identity=ident_b[:],
+                    )
+            nc.scalar.copy(out=gw[:, :, a * P : (a + 1) * P, :], in_=wt[:].rearrange("q c t r -> q c r t"))
 
         with tc.tile_pool(name="pre", bufs=1) as pre:
             xb = pre.tile([P, NP], BF16)
@@ -168,21 +185,8 @@ def tile_kanlinear_t_kernel(tc, x, coefficients, out):
             th = pre.tile([P, NP], F32, tag="rot", bufs=3)
             nc.scalar.activation(out=th[:], in_=xb[:], func=ACT.Tanh)
 
-            gw = wp.tile([P, 2, NO, 4], BF16, align_bytes=64, bufs=1)
-            for a in range(8):
-                cw = wp.tile([P, NI, 32], BF16)
-                nc.sync.dma_start(out=cw[:], in_=coef_v[a])
-                cw2 = wp.tile([P, 4, NI, 8], BF16)
-                nc.scalar.copy(out=cw2[:], in_=cw[:].rearrange("q i (t s) -> q t i s", s=8))
-                wt = psum.tile([P, 2, 4, P], BF16, tag="xt")
-                for c in range(2):
-                    for tq in range(4):
-                        nc.tensor.transpose(
-                            out=wt[:, c, tq, :],
-                            in_=cw2[:, tq, c * 16 : (c + 1) * 16, :].rearrange("q i s -> q (i s)"),
-                            identity=ident_b[:],
-                        )
-                nc.scalar.copy(out=gw[:, :, a * P : (a + 1) * P, :], in_=wt[:].rearrange("q c t r -> q c r t"))
+            for a in range(4):
+                weights_block(a)
 
             u0 = pre.tile([P, NP], F32, tag="rot", bufs=3)
             nc.vector.tensor_scalar(out=u0[:], in0=th[:], scalar1=31.5, scalar2=31.5, op0=ALU.mult, op1=ALU.add)
@@ -224,15 +228,15 @@ def tile_kanlinear_t_kernel(tc, x, coefficients, out):
             return arr[:, p0 : p0 + W2].rearrange("q (c g) -> q c g", g=4)
 
         def taylor_matrix():
-            lo_part = tb_hi[:, :, :, 0:8]
+            lo_part = tb_hi[:, :, 0:NLO]
             nc.vector.tensor_tensor(out=lo_part, in0=lo_part, in1=tb_lo[:], op=ALU.add)
             dmask = wp.tile([P, 32], F32, bufs=1)
             nc.vector.tensor_reduce(out=dmask[:], in_=ident_f[:].rearrange("q (p g) -> q p g", g=4), axis=AX.X, op=ALU.add)
             gmask = wp.tile([P, 4], F32, bufs=1)
             nc.vector.tensor_reduce(out=gmask[:], in_=ident_f[:].rearrange("q (p g) -> q g p", g=4), axis=AX.X, op=ALU.add)
             alt = wp.tile([P, 32], F32, bufs=1)
-            nc.vector.memset(alt[:, 0:16], 1.0)
-            nc.vector.memset(alt[:, 16:32], -1.0)
+            nc.vector.memset(alt[:], 1.0)
+            nc.vector.memset(alt[:, 1:32:2], -1.0)
             sa = wp.tile([P, 32], F32, bufs=1)
             nc.vector.tensor_tensor(out=sa[:], in0=dmask[:], in1=alt[:], op=ALU.mult)
             sgnp = wp.tile([P, 1], F32, bufs=1)
@@ -240,7 +244,7 @@ def tile_kanlinear_t_kernel(tc, x, coefficients, out):
             t1 = wp.tile([P, 12, 32], F32, bufs=1)
             nc.vector.tensor_tensor(
                 out=t1[:],
-                in0=tb_hi[:].rearrange("q r h s -> q r (h s)"),
+                in0=tb_hi[:],
                 in1=dmask[:].unsqueeze(1).to_broadcast([P, 12, 32]),
                 op=ALU.mult,
             )
@@ -265,25 +269,23 @@ def tile_kanlinear_t_kernel(tc, x, coefficients, out):
                     in_=gw[:, c, :, :].rearrange("q o t -> q (o t)"),
                 )
 
-        def powers_scalar(ph, duo, level):
+        def powers_scalar(ph, duo):
             hv = pair_view(hh, duo * W2)
-            if level == 0:
-                nc.scalar.activation(out=ph[:, :, 0, :], in_=hv, func=ACT.Identity, scale=0.0, bias=1.0)
-                nc.scalar.activation(out=ph[:, :, 1, :], in_=hv, func=ACT.Square)
-            else:
-                n = 1 << (level - 1)
-                nc.scalar.activation(out=ph[:, :, 2 * n : 4 * n : 2, :], in_=ph[:, :, n : 2 * n, :], func=ACT.Square)
-                nc.scalar.activation(out=ph[:, :, 2 * n + 1 : 4 * n : 2, :], in_=ph[:, :, 16 + n : 16 + 2 * n, :], func=ACT.Square)
+            nc.scalar.activation(out=ph[:, :, 0, :], in_=hv, func=ACT.Identity, scale=0.0, bias=1.0)
+            nc.scalar.copy(out=ph[:, :, 1, :], in_=hv)
 
-        def powers_vector(ph, duo, level):
-            lo = 0 if level == 0 else 1 << level
-            hi = 2 << level
-            nc.vector.tensor_tensor(
-                out=ph[:, :, 16 + lo : 16 + hi, :],
-                in0=ph[:, :, lo:hi, :],
-                in1=pair_view(hh, duo * W2).unsqueeze(2).to_broadcast([P, 16, hi - lo, 4]),
-                op=ALU.mult,
-            )
+        def powers_vector(ph):
+            n = 2
+            while n < 32:
+                half = n // 2
+                nc.vector.tensor_tensor(out=ph[:, :, n, :], in0=ph[:, :, half, :], in1=ph[:, :, half, :], op=ALU.mult)
+                nc.vector.tensor_tensor(
+                    out=ph[:, :, n + 1 : 2 * n, :],
+                    in0=ph[:, :, 1:n, :],
+                    in1=ph[:, :, n, :].unsqueeze(2).to_broadcast([P, 16, n - 1, 4]),
+                    op=ALU.mult,
+                )
+                n = 2 * n
 
         def pieces_a(ph, q):
             ft = psum.tile([P, 4, P], F32, tag="ft")
@@ -355,7 +357,7 @@ def tile_kanlinear_t_kernel(tc, x, coefficients, out):
             b_codes = work.tile([P, 2 * P], U32, tag="b_codes", align_bytes=64)
             b_scales = work.tile([P, 2 * P], U8, tag="b_scales", align_bytes=64)
             nc.vector.quantize_mx(out=b_codes[:].bitcast(FP8X4), scales=b_scales[:], in_=grouped[:].rearrange("q c r t -> q (c r t)"))
-            res = work.tile([P, NO], F32, tag="res", bufs=3)
+            res = work.tile([P, NO], F32, tag="res")
             for n in range(2):
                 acc = psum.tile([P, 512], F32, tag="acc")
                 for c in range(2):
@@ -371,63 +373,53 @@ def tile_kanlinear_t_kernel(tc, x, coefficients, out):
                 nc.scalar.copy(out=res[:, n * 512 : (n + 1) * 512], in_=acc[:])
             nc.sync.dma_start(out=out_v[t], in_=res[:])
 
+        ex = ctx.enter_context(tc.tile_pool(name="ex", bufs=2))
+        qq = ex.tile([P, 8, NP], F32, bufs=1)
+        cn = NP // 4
+
+        def outer_logs():
+            nc.scalar.activation(out=qq[:, 0, :], in_=hh[:], func=ACT.Relu, scale=-c31, bias=c31 * 0.5)
+            nc.scalar.activation(out=qq[:, 7, :], in_=hh[:], func=ACT.Relu, scale=c31, bias=c31 * 0.5)
+            for m in range(1, 4):
+                nc.scalar.activation(out=qq[:, m, :], in_=hh[:], func=ACT.Ln, scale=-c31, bias=c31 * (m + 0.5))
+                nc.scalar.activation(out=qq[:, 7 - m, :], in_=hh[:], func=ACT.Ln, scale=c31, bias=c31 * (m + 0.5))
+            nc.scalar.activation(out=qq[:, mirror_rows(0), :], in_=qq[:, mirror_rows(0), :], func=ACT.Ln, bias=1.0e-18)
+
+        def outer_scalar(ch):
+            qc = qq[:, :, ch * cn : (ch + 1) * cn]
+            nc.scalar.activation(out=qc, in_=qc, func=ACT.Exp, scale=31.0)
+            nc.scalar.copy(out=xe[:, mirror_rows(0), ch * cn : (ch + 1) * cn], in_=qc[:, mirror_rows(0), :])
+
+        def outer_vector(ch):
+            qc = qq[:, :, ch * cn : (ch + 1) * cn]
+            xec = xe[:, :, ch * cn : (ch + 1) * cn]
+            nc.vector.scalar_tensor_tensor(out=xec[:, mirror_rows(1), :], in0=qc[:, mirror_rows(0), :], scalar=-32.0, in1=qc[:, mirror_rows(1), :], op0=ALU.mult, op1=ALU.add)
+            ta = ex.tile([P, 2, cn], F32, tag="ta")
+            nc.vector.scalar_tensor_tensor(out=ta[:], in0=qc[:, mirror_rows(1), :], scalar=-32.0, in1=qc[:, mirror_rows(2), :], op0=ALU.mult, op1=ALU.add)
+            nc.vector.scalar_tensor_tensor(out=xec[:, mirror_rows(2), :], in0=qc[:, mirror_rows(0), :], scalar=496.0, in1=ta[:], op0=ALU.mult, op1=ALU.add)
+            tb3 = ex.tile([P, 2, cn], F32, tag="tb3")
+            nc.vector.scalar_tensor_tensor(out=tb3[:], in0=qc[:, mirror_rows(2), :], scalar=-32.0, in1=qc[:, mirror_rows(3), :], op0=ALU.mult, op1=ALU.add)
+            tc3 = ex.tile([P, 2, cn], F32, tag="tc3")
+            nc.vector.scalar_tensor_tensor(out=tc3[:], in0=qc[:, mirror_rows(1), :], scalar=496.0, in1=tb3[:], op0=ALU.mult, op1=ALU.add)
+            nc.vector.scalar_tensor_tensor(out=xec[:, mirror_rows(3), :], in0=qc[:, mirror_rows(0), :], scalar=-4960.0, in1=tc3[:], op0=ALU.mult, op1=ALU.add)
+
         ph_of = {}
         for duo in range(2):
             ph_new = work.tile([P, 16, 32, 4], F32, tag="ph")
             ph_of[duo] = ph_new
-            for level in range(4):
-                powers_scalar(ph_new, duo, level)
-                powers_vector(ph_new, duo, level)
-
-        with tc.tile_pool(name="ex", bufs=2) as ex:
-            cn = 64
-            nch = NP // cn
-            qq_of = {}
-            for ch in range(nch + 1):
-                if ch < nch:
-                    c0 = ch * cn
-                    xs1 = ex.tile([P, 8, cn], F32, tag="xs1")
-                    for m in range(4):
-                        nc.scalar.activation(out=xs1[:, m, :], in_=hh[:, c0 : c0 + cn], func=ACT.Identity, scale=-c31, bias=c31 * (m + 0.5))
-                        nc.scalar.activation(out=xs1[:, 7 - m, :], in_=hh[:, c0 : c0 + cn], func=ACT.Identity, scale=c31, bias=c31 * (m + 0.5))
-                    xs2 = ex.tile([P, 8, cn], F32, tag="xs2")
-                    nc.scalar.activation(out=xs2[:], in_=xs1[:], func=ACT.Square)
-                    xs4 = ex.tile([P, 8, cn], F32, tag="xs4")
-                    nc.scalar.activation(out=xs4[:], in_=xs2[:], func=ACT.Square)
-                    xs8 = ex.tile([P, 8, cn], F32, tag="xs8")
-                    nc.scalar.activation(out=xs8[:], in_=xs4[:], func=ACT.Square)
-                    xs16 = ex.tile([P, 8, cn], F32, tag="xs16")
-                    nc.scalar.activation(out=xs16[:], in_=xs8[:], func=ACT.Square)
-                if ch > 0:
-                    prev = (ch - 1) * cn
-                    nc.scalar.copy(out=xe[:, mirror_rows(0), prev : prev + cn], in_=qq_of[ch - 1][:, mirror_rows(0), :])
-                if ch < nch:
-                    pr1 = ex.tile([P, 8, cn], F32, tag="pr1")
-                    nc.vector.tensor_tensor(out=pr1[:], in0=xs1[:], in1=xs2[:], op=ALU.mult)
-                    pr2 = ex.tile([P, 8, cn], F32, tag="pr2")
-                    nc.vector.tensor_tensor(out=pr2[:], in0=xs4[:], in1=xs8[:], op=ALU.mult)
-                    pr3 = ex.tile([P, 8, cn], F32, tag="pr3")
-                    nc.vector.tensor_tensor(out=pr3[:], in0=pr1[:], in1=pr2[:], op=ALU.mult)
-                    qq = ex.tile([P, 8, cn], F32, tag="qq")
-                    qq_of[ch] = qq
-                    nc.vector.tensor_tensor(out=qq[:], in0=pr3[:], in1=xs16[:], op=ALU.mult)
-                    xec = xe[:, :, c0 : c0 + cn]
-                    nc.vector.scalar_tensor_tensor(out=xec[:, mirror_rows(1), :], in0=qq[:, mirror_rows(0), :], scalar=-32.0, in1=qq[:, mirror_rows(1), :], op0=ALU.mult, op1=ALU.add)
-                    ta = ex.tile([P, 2, cn], F32, tag="ta")
-                    nc.vector.scalar_tensor_tensor(out=ta[:], in0=qq[:, mirror_rows(1), :], scalar=-32.0, in1=qq[:, mirror_rows(2), :], op0=ALU.mult, op1=ALU.add)
-                    nc.vector.scalar_tensor_tensor(out=xec[:, mirror_rows(2), :], in0=qq[:, mirror_rows(0), :], scalar=496.0, in1=ta[:], op0=ALU.mult, op1=ALU.add)
-                    tb3 = ex.tile([P, 2, cn], F32, tag="tb3")
-                    nc.vector.scalar_tensor_tensor(out=tb3[:], in0=qq[:, mirror_rows(2), :], scalar=-32.0, in1=qq[:, mirror_rows(3), :], op0=ALU.mult, op1=ALU.add)
-                    tc3 = ex.tile([P, 2, cn], F32, tag="tc3")
-                    nc.vector.scalar_tensor_tensor(out=tc3[:], in0=qq[:, mirror_rows(1), :], scalar=496.0, in1=tb3[:], op0=ALU.mult, op1=ALU.add)
-                    nc.vector.scalar_tensor_tensor(out=xec[:, mirror_rows(3), :], in0=qq[:, mirror_rows(0), :], scalar=-4960.0, in1=tc3[:], op0=ALU.mult, op1=ALU.add)
-                if ch == 11:
-                    taylor_matrix()
-        quantise_weights()
-
+            powers_scalar(ph_new, duo)
+        taylor_matrix()
+        powers_vector(ph_of[0])
+        outer_logs()
+        outer_scalar(0)
+        powers_vector(ph_of[1])
+        outer_vector(0)
         at_cur = work.tile([P, 32, W2], BF16, tag="at")
+        fts_next = pieces_a(ph_of[0], 0)
         for q in range(4):
-            fts = pieces_a(ph_of[0], q)
+            fts = fts_next
+            if q < 3:
+                fts_next = pieces_a(ph_of[0], q + 1)
             pa = pieces_b(fts)
             pieces_c(at_cur, pa, q)
         pieces_outer(at_cur, 0)
@@ -438,10 +430,6 @@ def tile_kanlinear_t_kernel(tc, x, coefficients, out):
             finishing = n >= 1
             piecing = n + 1 < ND
             powering = n + 2 < ND
-            if powering:
-                ph_new = work.tile([P, 16, 32, 4], F32, tag="ph")
-                ph_of[n + 2] = ph_new
-                powers_scalar(ph_new, n + 2, 0)
             if finishing:
                 yc0 = turn_a(yfin_prev, 0)
             if piecing:
@@ -456,9 +444,8 @@ def tile_kanlinear_t_kernel(tc, x, coefficients, out):
                 grouped0 = turn_c(xt0)
             if shifting:
                 ycur = shift_stage(n, 4, at_cur)
-            if powering:
-                powers_vector(ph_new, n + 2, 0)
-                powers_scalar(ph_new, n + 2, 1)
+            if n == 1:
+                quantise_weights()
             if piecing:
                 pieces_c(at_next, pa0, 0)
                 fts1 = pieces_a(ph_of[n + 1], 1)
@@ -472,30 +459,32 @@ def tile_kanlinear_t_kernel(tc, x, coefficients, out):
                 pieces_c(at_next, pa1, 1)
             if shifting:
                 ycur = shift_stage(n, 3, ycur)
-            if powering:
-                powers_vector(ph_new, n + 2, 1)
-                powers_scalar(ph_new, n + 2, 2)
+                ycur = shift_stage(n, 2, ycur)
             if piecing:
                 for q in (2, 3):
                     fts = pieces_a(ph_of[n + 1], q)
                     pa = pieces_b(fts)
                     pieces_c(at_next, pa, q)
-            if shifting:
-                ycur = shift_stage(n, 2, ycur)
-            if powering:
-                powers_vector(ph_new, n + 2, 2)
-                powers_scalar(ph_new, n + 2, 3)
-            if piecing:
                 pieces_outer(at_next, n + 1)
-            if shifting:
-                ycur = shift_stage(n, 1, ycur)
+            if 1 <= n <= 3:
+                outer_scalar(n)
             if powering:
-                powers_vector(ph_new, n + 2, 3)
-            if shifting:
-                ycur = shift_stage(n, 0, ycur)
+                ph_new = work.tile([P, 16, 32, 4], F32, tag="ph")
+                ph_of[n + 2] = ph_new
+                powers_scalar(ph_new, n + 2)
+            if n == 0:
+                for a in range(4, 8):
+                    weights_block(a)
             if finishing:
                 multiply(2 * (n - 1), grouped0)
                 multiply(2 * (n - 1) + 1, grouped1)
+            if shifting:
+                ycur = shift_stage(n, 1, ycur)
+                ycur = shift_stage(n, 0, ycur)
+            if powering:
+                powers_vector(ph_new)
+            if 1 <= n <= 3:
+                outer_vector(n)
             if shifting:
                 yfin_prev = ycur
             if piecing:

@@ -22,6 +22,7 @@ NO = 1024
 NT = NB // P
 NP = NT * NI
 ND = NT // 2
+NQ = ND // 2
 W2 = 2 * NI
 ROWS = 80
 UMAX = 62.99999
@@ -129,7 +130,6 @@ def tile_kanlinear_t_kernel(tc, x, coefficients, out):
         ctx.enter_context(tc.manual_schedule())
         keep = ctx.enter_context(tc.tile_pool(name="keep", bufs=1))
         psum = ctx.enter_context(tc.psum_pool(name="psum", bufs=2))
-        work = ctx.enter_context(tc.tile_pool(name="work", bufs=2))
         wp = ctx.enter_context(tc.tile_pool(name="wp", bufs=2))
 
         ident_f = keep.tile([P, P], F32)
@@ -168,7 +168,10 @@ def tile_kanlinear_t_kernel(tc, x, coefficients, out):
             cw = wp.tile([P, NI, 32], BF16, tag="cw")
             nc.sync.dma_start(out=cw[:], in_=coef_v[a])
             cw2 = wp.tile([P, 4, NI, 8], BF16, tag="cw2")
-            nc.scalar.copy(out=cw2[:], in_=cw[:].rearrange("q i (t s) -> q t i s", s=8))
+            if a < 4:
+                nc.scalar.copy(out=cw2[:], in_=cw[:].rearrange("q i (t s) -> q t i s", s=8))
+            else:
+                nc.gpsimd.tensor_scalar(out=cw2[:], in0=cw[:].rearrange("q i (t s) -> q t i s", s=8), scalar1=1.0, scalar2=0.0, op0=ALU.mult, op1=ALU.add)
             wt = psum.tile([P, 2, 4, P], BF16, tag="xt")
             for c in range(2):
                 for tq in range(4):
@@ -224,6 +227,8 @@ def tile_kanlinear_t_kernel(tc, x, coefficients, out):
             nc.vector.tensor_scalar_mul(out=mr_neg[:], in0=mr_pos[:], scalar1=-1.0)
             nc.vector.tensor_scalar_mul(out=ml_neg[:], in0=ml_pos[:], scalar1=-1.0)
 
+        work = ctx.enter_context(tc.tile_pool(name="work", bufs=2))
+
         def pair_view(arr, p0):
             return arr[:, p0 : p0 + W2].rearrange("q (c g) -> q c g", g=4)
 
@@ -269,23 +274,26 @@ def tile_kanlinear_t_kernel(tc, x, coefficients, out):
                     in_=gw[:, c, :, :].rearrange("q o t -> q (o t)"),
                 )
 
-        def powers_scalar(ph, duo):
+        def powers_scalar(duo):
+            ph = work.tile([P, 16, 32, 4], F32, tag="ph")
+            pw = work.tile([P, 16, 4, 4], F32, tag="pw")
             hv = pair_view(hh, duo * W2)
             nc.scalar.activation(out=ph[:, :, 0, :], in_=hv, func=ACT.Identity, scale=0.0, bias=1.0)
             nc.scalar.copy(out=ph[:, :, 1, :], in_=hv)
+            nc.scalar.activation(out=pw[:, :, 0, :], in_=hv, func=ACT.Square)
+            for lv in range(1, 4):
+                nc.scalar.activation(out=pw[:, :, lv, :], in_=pw[:, :, lv - 1, :], func=ACT.Square)
+            return (ph, pw)
 
-        def powers_vector(ph):
-            n = 2
-            while n < 32:
-                half = n // 2
-                nc.vector.tensor_tensor(out=ph[:, :, n, :], in0=ph[:, :, half, :], in1=ph[:, :, half, :], op=ALU.mult)
-                nc.vector.tensor_tensor(
-                    out=ph[:, :, n + 1 : 2 * n, :],
-                    in0=ph[:, :, 1:n, :],
-                    in1=ph[:, :, n, :].unsqueeze(2).to_broadcast([P, 16, n - 1, 4]),
-                    op=ALU.mult,
-                )
-                n = 2 * n
+        def powers_step(php, lv):
+            ph, pw = php
+            n = 2 << lv
+            nc.vector.tensor_tensor(
+                out=ph[:, :, n : 2 * n, :],
+                in0=ph[:, :, 0:n, :],
+                in1=pw[:, :, lv, :].unsqueeze(2).to_broadcast([P, 16, n, 4]),
+                op=ALU.mult,
+            )
 
         def pieces_a(ph, q):
             ft = psum.tile([P, 4, P], F32, tag="ft")
@@ -311,11 +319,11 @@ def tile_kanlinear_t_kernel(tc, x, coefficients, out):
             nc.scalar.copy(out=at[:, 0:4, :], in_=xe[:, 0:4, duo * W2 : (duo + 1) * W2])
             nc.scalar.copy(out=at[:, 28:32, :], in_=xe[:, 4:8, duo * W2 : (duo + 1) * W2])
 
-        def shift_stage(duo, k, src):
+        def shift_sign(chain, duo, k, src):
             p0 = duo * W2
             a = 1 << k
             out_lo = 32 - a if k > 0 else 32
-            gcur = work.tile([P, ROWS, W2], BF16, tag="gs")
+            gcur = work.tile([P, ROWS, W2], BF16, tag="gs%s" % chain, bufs=1)
             if k == 4:
                 for off, m_pos, m_neg in ((0, ml_pos, ml_neg), (32, mr_pos, mr_neg)):
                     for row, mm in ((0, m_pos), (16, m_neg)):
@@ -325,11 +333,16 @@ def tile_kanlinear_t_kernel(tc, x, coefficients, out):
                 for want, mu in ((1, mu_pos[k]), (-1, mu_neg[k])):
                     for grp in row_groups(out_lo - a, 64, lambda e: chi(k + 1, e) * chi(k, e), want):
                         nc.vector.tensor_tensor(out=rows_view(gcur, grp, 0), in0=rows_view(src, grp, 0), in1=pair_rows(mu, p0, grp), op=ALU.mult)
+            return gcur
+
+        def shift_pick(chain, k, gcur):
+            a = 1 << k
+            out_lo = 32 - a if k > 0 else 32
             if k > 0:
-                ycur = work.tile([P, ROWS, W2], BF16, tag="ys")
+                ycur = work.tile([P, ROWS, W2], BF16, tag="ys%s" % chain, bufs=1)
                 base = 0
             else:
-                ycur = work.tile([P, 34, W2], BF16, tag="yfin")
+                ycur = work.tile([P, 34, W2], BF16, tag="yfin%s" % chain)
                 base = 32
             for want, op in ((1, ALU.max), (-1, ALU.min)):
                 for grp in row_groups(out_lo, 64, lambda e: chi(k, e), want):
@@ -349,14 +362,18 @@ def tile_kanlinear_t_kernel(tc, x, coefficients, out):
             return xt
 
         def turn_c(xt):
-            grouped = work.tile([P, 2, P, 4], BF16, tag="grouped", align_bytes=64)
+            grouped = work.tile([P, 2, P, 4], BF16, tag="grouped", align_bytes=64, bufs=4)
             nc.scalar.copy(out=grouped[:], in_=xt[:].rearrange("q c t r -> q c r t"))
             return grouped
 
-        def multiply(t, grouped):
-            b_codes = work.tile([P, 2 * P], U32, tag="b_codes", align_bytes=64)
-            b_scales = work.tile([P, 2 * P], U8, tag="b_scales", align_bytes=64)
+        def quantise(grouped):
+            b_codes = work.tile([P, 2 * P], U32, tag="b_codes", align_bytes=64, bufs=4)
+            b_scales = work.tile([P, 2 * P], U8, tag="b_scales", align_bytes=64, bufs=4)
             nc.vector.quantize_mx(out=b_codes[:].bitcast(FP8X4), scales=b_scales[:], in_=grouped[:].rearrange("q c r t -> q (c r t)"))
+            return (b_codes, b_scales)
+
+        def multiply(t, operand):
+            b_codes, b_scales = operand
             res = work.tile([P, NO], F32, tag="res")
             for n in range(2):
                 acc = psum.tile([P, 512], F32, tag="acc")
@@ -373,119 +390,210 @@ def tile_kanlinear_t_kernel(tc, x, coefficients, out):
                 nc.scalar.copy(out=res[:, n * 512 : (n + 1) * 512], in_=acc[:])
             nc.sync.dma_start(out=out_v[t], in_=res[:])
 
-        ex = ctx.enter_context(tc.tile_pool(name="ex", bufs=2))
-        qq = ex.tile([P, 8, NP], F32, bufs=1)
+        def pieces(duo, php, chain):
+            at = work.tile([P, 32, W2], BF16, tag="at%s" % chain)
+            fts_next = pieces_a(php[0], 0)
+            for q in range(4):
+                fts = fts_next
+                if q < 3:
+                    fts_next = pieces_a(php[0], q + 1)
+                pa = pieces_b(fts)
+                pieces_c(at, pa, q)
+            pieces_outer(at, duo)
+            return at
+
+        ex = ctx.enter_context(tc.tile_pool(name="ex", bufs=1))
+        hn = NP // 2
         cn = NP // 4
 
-        def outer_logs():
-            nc.scalar.activation(out=qq[:, 0, :], in_=hh[:], func=ACT.Relu, scale=-c31, bias=c31 * 0.5)
-            nc.scalar.activation(out=qq[:, 7, :], in_=hh[:], func=ACT.Relu, scale=c31, bias=c31 * 0.5)
+        def outer_logs(half):
+            qq = ex.tile([P, 8, hn], F32, tag="qq")
+            hv = hh[:, half * hn : (half + 1) * hn]
+            nc.scalar.activation(out=qq[:, 0, :], in_=hv, func=ACT.Relu, scale=-c31, bias=c31 * 0.5)
+            nc.scalar.activation(out=qq[:, 7, :], in_=hv, func=ACT.Relu, scale=c31, bias=c31 * 0.5)
             for m in range(1, 4):
-                nc.scalar.activation(out=qq[:, m, :], in_=hh[:], func=ACT.Ln, scale=-c31, bias=c31 * (m + 0.5))
-                nc.scalar.activation(out=qq[:, 7 - m, :], in_=hh[:], func=ACT.Ln, scale=c31, bias=c31 * (m + 0.5))
+                nc.scalar.activation(out=qq[:, m, :], in_=hv, func=ACT.Ln, scale=-c31, bias=c31 * (m + 0.5))
+                nc.scalar.activation(out=qq[:, 7 - m, :], in_=hv, func=ACT.Ln, scale=c31, bias=c31 * (m + 0.5))
             nc.scalar.activation(out=qq[:, mirror_rows(0), :], in_=qq[:, mirror_rows(0), :], func=ACT.Ln, bias=1.0e-18)
+            return qq
 
-        def outer_scalar(ch):
-            qc = qq[:, :, ch * cn : (ch + 1) * cn]
+        def outer_scalar(qq, ch):
+            qc = qq[:, :, (ch % 2) * cn : (ch % 2 + 1) * cn]
             nc.scalar.activation(out=qc, in_=qc, func=ACT.Exp, scale=31.0)
             nc.scalar.copy(out=xe[:, mirror_rows(0), ch * cn : (ch + 1) * cn], in_=qc[:, mirror_rows(0), :])
 
-        def outer_vector(ch):
-            qc = qq[:, :, ch * cn : (ch + 1) * cn]
+        def outer_vector(qq, ch):
+            qc = qq[:, :, (ch % 2) * cn : (ch % 2 + 1) * cn]
             xec = xe[:, :, ch * cn : (ch + 1) * cn]
-            nc.vector.scalar_tensor_tensor(out=xec[:, mirror_rows(1), :], in0=qc[:, mirror_rows(0), :], scalar=-32.0, in1=qc[:, mirror_rows(1), :], op0=ALU.mult, op1=ALU.add)
             ta = ex.tile([P, 2, cn], F32, tag="ta")
-            nc.vector.scalar_tensor_tensor(out=ta[:], in0=qc[:, mirror_rows(1), :], scalar=-32.0, in1=qc[:, mirror_rows(2), :], op0=ALU.mult, op1=ALU.add)
-            nc.vector.scalar_tensor_tensor(out=xec[:, mirror_rows(2), :], in0=qc[:, mirror_rows(0), :], scalar=496.0, in1=ta[:], op0=ALU.mult, op1=ALU.add)
             tb3 = ex.tile([P, 2, cn], F32, tag="tb3")
-            nc.vector.scalar_tensor_tensor(out=tb3[:], in0=qc[:, mirror_rows(2), :], scalar=-32.0, in1=qc[:, mirror_rows(3), :], op0=ALU.mult, op1=ALU.add)
             tc3 = ex.tile([P, 2, cn], F32, tag="tc3")
+            nc.vector.scalar_tensor_tensor(out=ta[:], in0=qc[:, mirror_rows(1), :], scalar=-32.0, in1=qc[:, mirror_rows(2), :], op0=ALU.mult, op1=ALU.add)
+            nc.vector.scalar_tensor_tensor(out=tb3[:], in0=qc[:, mirror_rows(2), :], scalar=-32.0, in1=qc[:, mirror_rows(3), :], op0=ALU.mult, op1=ALU.add)
+            nc.vector.scalar_tensor_tensor(out=xec[:, mirror_rows(1), :], in0=qc[:, mirror_rows(0), :], scalar=-32.0, in1=qc[:, mirror_rows(1), :], op0=ALU.mult, op1=ALU.add)
             nc.vector.scalar_tensor_tensor(out=tc3[:], in0=qc[:, mirror_rows(1), :], scalar=496.0, in1=tb3[:], op0=ALU.mult, op1=ALU.add)
+            nc.vector.scalar_tensor_tensor(out=xec[:, mirror_rows(2), :], in0=qc[:, mirror_rows(0), :], scalar=496.0, in1=ta[:], op0=ALU.mult, op1=ALU.add)
             nc.vector.scalar_tensor_tensor(out=xec[:, mirror_rows(3), :], in0=qc[:, mirror_rows(0), :], scalar=-4960.0, in1=tc3[:], op0=ALU.mult, op1=ALU.add)
 
-        ph_of = {}
-        for duo in range(2):
-            ph_new = work.tile([P, 16, 32, 4], F32, tag="ph")
-            ph_of[duo] = ph_new
-            powers_scalar(ph_new, duo)
+        php_a = powers_scalar(0)
+        php_b = powers_scalar(1)
         taylor_matrix()
-        powers_vector(ph_of[0])
-        outer_logs()
-        outer_scalar(0)
-        powers_vector(ph_of[1])
-        outer_vector(0)
-        at_cur = work.tile([P, 32, W2], BF16, tag="at")
-        fts_next = pieces_a(ph_of[0], 0)
-        for q in range(4):
-            fts = fts_next
-            if q < 3:
-                fts_next = pieces_a(ph_of[0], q + 1)
-            pa = pieces_b(fts)
-            pieces_c(at_cur, pa, q)
-        pieces_outer(at_cur, 0)
+        for lv in range(4):
+            powers_step(php_a, lv)
+            powers_step(php_b, lv)
+        qq_cur = outer_logs(0)
+        outer_scalar(qq_cur, 0)
+        outer_vector(qq_cur, 0)
+        at_a = pieces(0, php_a, "a")
+        php_a = powers_scalar(2)
+        for lv in range(4):
+            powers_step(php_a, lv)
+        at_b = pieces(1, php_b, "b")
+        php_b = powers_scalar(3)
 
-        yfin_prev = None
-        for n in range(ND + 1):
-            shifting = n < ND
-            finishing = n >= 1
-            piecing = n + 1 < ND
-            powering = n + 2 < ND
+        fin_a = None
+        fin_b = None
+        for m in range(NQ + 1):
+            shifting = m < NQ
+            finishing = m >= 1
+            preparing = m + 1 < NQ
+            ahead = m + 2 < NQ
+            da = 2 * m
+            db = 2 * m + 1
+            t0 = 4 * (m - 1)
+            old_a = at_a
+            old_b = at_b
+            if m == 0:
+                outer_scalar(qq_cur, 1)
             if finishing:
-                yc0 = turn_a(yfin_prev, 0)
-            if piecing:
-                at_next = work.tile([P, 32, W2], BF16, tag="at")
-                fts0 = pieces_a(ph_of[n + 1], 0)
+                yc0 = turn_a(fin_a, 0)
+            if preparing:
+                at_a = work.tile([P, 32, W2], BF16, tag="ata")
+                f0 = pieces_a(php_a[0], 0)
             if finishing:
+                yc1 = turn_a(fin_a, 1)
                 xt0 = turn_b(yc0)
-            if piecing:
-                pa0 = pieces_b(fts0)
+            if preparing:
+                f1 = pieces_a(php_a[0], 1)
+                p0 = pieces_b(f0)
             if finishing:
-                yc1 = turn_a(yfin_prev, 1)
                 grouped0 = turn_c(xt0)
             if shifting:
-                ycur = shift_stage(n, 4, at_cur)
-            if n == 1:
+                ga = shift_sign("a", da, 4, old_a)
+                gb = shift_sign("b", db, 4, old_b)
+            if preparing:
+                powers_step(php_b, 0)
+            if m == 1:
                 quantise_weights()
-            if piecing:
-                pieces_c(at_next, pa0, 0)
-                fts1 = pieces_a(ph_of[n + 1], 1)
+            if shifting:
+                ya = shift_pick("a", 4, ga)
+                yb = shift_pick("b", 4, gb)
+            if preparing:
+                powers_step(php_b, 1)
+            if finishing:
+                op0 = quantise(grouped0)
+            if preparing:
+                pieces_c(at_a, p0, 0)
             if finishing:
                 xt1 = turn_b(yc1)
-            if piecing:
-                pa1 = pieces_b(fts1)
+            if preparing:
+                p1 = pieces_b(f1)
+            if finishing:
+                yc2 = turn_a(fin_b, 0)
+            if preparing:
+                f2 = pieces_a(php_a[0], 2)
             if finishing:
                 grouped1 = turn_c(xt1)
-            if piecing:
-                pieces_c(at_next, pa1, 1)
+                multiply(t0, op0)
+            if preparing:
+                pieces_c(at_a, p1, 1)
             if shifting:
-                ycur = shift_stage(n, 3, ycur)
-                ycur = shift_stage(n, 2, ycur)
-            if piecing:
-                for q in (2, 3):
-                    fts = pieces_a(ph_of[n + 1], q)
-                    pa = pieces_b(fts)
-                    pieces_c(at_next, pa, q)
-                pieces_outer(at_next, n + 1)
-            if 1 <= n <= 3:
-                outer_scalar(n)
-            if powering:
-                ph_new = work.tile([P, 16, 32, 4], F32, tag="ph")
-                ph_of[n + 2] = ph_new
-                powers_scalar(ph_new, n + 2)
-            if n == 0:
+                ga = shift_sign("a", da, 3, ya)
+                gb = shift_sign("b", db, 3, yb)
+            if preparing:
+                powers_step(php_b, 2)
+            if finishing:
+                op1 = quantise(grouped1)
+            if shifting:
+                ya = shift_pick("a", 3, ga)
+                yb = shift_pick("b", 3, gb)
+            if preparing:
+                powers_step(php_b, 3)
+            if finishing:
+                xt2 = turn_b(yc2)
+            if preparing:
+                p2 = pieces_b(f2)
+            if finishing:
+                yc3 = turn_a(fin_b, 1)
+            if preparing:
+                f3 = pieces_a(php_a[0], 3)
+            if finishing:
+                grouped2 = turn_c(xt2)
+            if preparing:
+                pieces_c(at_a, p2, 2)
+            if finishing:
+                multiply(t0 + 1, op1)
+                xt3 = turn_b(yc3)
+            if preparing:
+                p3 = pieces_b(f3)
+            if finishing:
+                grouped3 = turn_c(xt3)
+            if preparing:
+                pieces_c(at_a, p3, 3)
+                pieces_outer(at_a, da + 2)
+            if ahead:
+                php_a = powers_scalar(da + 4)
+            if shifting:
+                ga = shift_sign("a", da, 2, ya)
+                gb = shift_sign("b", db, 2, yb)
+            if finishing:
+                op2 = quantise(grouped2)
+            if shifting:
+                ya = shift_pick("a", 2, ga)
+                yb = shift_pick("b", 2, gb)
+            if finishing:
+                op3 = quantise(grouped3)
+            if m == 0 or m == 2 or m == 3:
+                outer_vector(qq_cur, 1 if m == 0 else m)
+            if preparing:
+                at_b = work.tile([P, 32, W2], BF16, tag="atb")
+                f0 = pieces_a(php_b[0], 0)
+                f1 = pieces_a(php_b[0], 1)
+                p0 = pieces_b(f0)
+            if finishing:
+                multiply(t0 + 2, op2)
+            if preparing:
+                pieces_c(at_b, p0, 0)
+                p1 = pieces_b(f1)
+                f2 = pieces_a(php_b[0], 2)
+                pieces_c(at_b, p1, 1)
+            if finishing:
+                multiply(t0 + 3, op3)
+            if preparing:
+                p2 = pieces_b(f2)
+                f3 = pieces_a(php_b[0], 3)
+                pieces_c(at_b, p2, 2)
+                p3 = pieces_b(f3)
+                pieces_c(at_b, p3, 3)
+                pieces_outer(at_b, db + 2)
+            if ahead:
+                php_b = powers_scalar(db + 4)
+            if m == 0:
+                qq_cur = outer_logs(1)
                 for a in range(4, 8):
                     weights_block(a)
-            if finishing:
-                multiply(2 * (n - 1), grouped0)
-                multiply(2 * (n - 1) + 1, grouped1)
-            if shifting:
-                ycur = shift_stage(n, 1, ycur)
-                ycur = shift_stage(n, 0, ycur)
-            if powering:
-                powers_vector(ph_new)
-            if 1 <= n <= 3:
-                outer_vector(n)
-            if shifting:
-                yfin_prev = ycur
-            if piecing:
-                at_cur = at_next
+            if m == 1 or m == 2:
+                outer_scalar(qq_cur, m + 1)
+            for k in (1, 0):
+                if shifting:
+                    ga = shift_sign("a", da, k, ya)
+                    gb = shift_sign("b", db, k, yb)
+                if ahead:
+                    powers_step(php_a, 2 - 2 * k)
+                if shifting:
+                    ya = shift_pick("a", k, ga)
+                    yb = shift_pick("b", k, gb)
+                if ahead:
+                    powers_step(php_a, 3 - 2 * k)
+            fin_a = ya
+            fin_b = yb

@@ -26,6 +26,8 @@ NQ = ND // 2
 W2 = 2 * NI
 ROWS = 80
 UMAX = 62.99999
+NPW = 16
+NG = P // NPW
 NLO = 8
 
 
@@ -137,7 +139,7 @@ def tile_kanlinear_t_kernel(tc, x, coefficients, out):
         ident_b = keep.tile([P, P], BF16)
         make_identity(nc, ident_b[:])
 
-        wmat = keep.tile([P, 24, 4], F32)
+        wmat = keep.tile([P, 24, NG], F32)
         w_codes = keep.tile([P, 2, NO], U32, align_bytes=64)
         w_scales = keep.tile([P, 2, NO], U8, align_bytes=64)
         hh = keep.tile([P, NP], F32)
@@ -152,9 +154,9 @@ def tile_kanlinear_t_kernel(tc, x, coefficients, out):
         mr_neg = keep.tile([P, NP], BF16)
         xe = keep.tile([P, 8, NP], BF16)
 
-        tb_hi = keep.tile([P, 12, 32], F32)
+        tb_hi = keep.tile([P, 12, NPW], F32)
         tb_lo = keep.tile([P, 12, NLO], F32)
-        for p in range(32):
+        for p in range(NPW):
             for r in range(4, 16):
                 v = taylor_coefficient(r, p)
                 hi = to_float32(v)
@@ -230,27 +232,27 @@ def tile_kanlinear_t_kernel(tc, x, coefficients, out):
         work = ctx.enter_context(tc.tile_pool(name="work", bufs=2))
 
         def pair_view(arr, p0):
-            return arr[:, p0 : p0 + W2].rearrange("q (c g) -> q c g", g=4)
+            return arr[:, p0 : p0 + W2].rearrange("q (c g) -> q c g", g=NG)
 
         def taylor_matrix():
             lo_part = tb_hi[:, :, 0:NLO]
             nc.vector.tensor_tensor(out=lo_part, in0=lo_part, in1=tb_lo[:], op=ALU.add)
-            dmask = wp.tile([P, 32], F32, bufs=1)
-            nc.vector.tensor_reduce(out=dmask[:], in_=ident_f[:].rearrange("q (p g) -> q p g", g=4), axis=AX.X, op=ALU.add)
-            gmask = wp.tile([P, 4], F32, bufs=1)
-            nc.vector.tensor_reduce(out=gmask[:], in_=ident_f[:].rearrange("q (p g) -> q g p", g=4), axis=AX.X, op=ALU.add)
-            alt = wp.tile([P, 32], F32, bufs=1)
+            dmask = wp.tile([P, NPW], F32, bufs=1)
+            nc.vector.tensor_reduce(out=dmask[:], in_=ident_f[:].rearrange("q (p g) -> q p g", g=NG), axis=AX.X, op=ALU.add)
+            gmask = wp.tile([P, NG], F32, bufs=1)
+            nc.vector.tensor_reduce(out=gmask[:], in_=ident_f[:].rearrange("q (p g) -> q g p", g=NG), axis=AX.X, op=ALU.add)
+            alt = wp.tile([P, NPW], F32, bufs=1)
             nc.vector.memset(alt[:], 1.0)
-            nc.vector.memset(alt[:, 1:32:2], -1.0)
-            sa = wp.tile([P, 32], F32, bufs=1)
+            nc.vector.memset(alt[:, 1:NPW:2], -1.0)
+            sa = wp.tile([P, NPW], F32, bufs=1)
             nc.vector.tensor_tensor(out=sa[:], in0=dmask[:], in1=alt[:], op=ALU.mult)
             sgnp = wp.tile([P, 1], F32, bufs=1)
             nc.vector.tensor_reduce(out=sgnp[:], in_=sa[:], axis=AX.X, op=ALU.add)
-            t1 = wp.tile([P, 12, 32], F32, bufs=1)
+            t1 = wp.tile([P, 12, NPW], F32, bufs=1)
             nc.vector.tensor_tensor(
                 out=t1[:],
                 in0=tb_hi[:],
-                in1=dmask[:].unsqueeze(1).to_broadcast([P, 12, 32]),
+                in1=dmask[:].unsqueeze(1).to_broadcast([P, 12, NPW]),
                 op=ALU.mult,
             )
             w0 = wp.tile([P, 12], F32, bufs=1)
@@ -261,8 +263,8 @@ def tile_kanlinear_t_kernel(tc, x, coefficients, out):
                 nc.vector.tensor_copy(out=wc[:, e - 4 : e - 3], in_=w0[:, 27 - e : 28 - e])
             nc.vector.tensor_tensor(
                 out=wmat[:],
-                in0=wc[:].unsqueeze(2).to_broadcast([P, 24, 4]),
-                in1=gmask[:].unsqueeze(1).to_broadcast([P, 24, 4]),
+                in0=wc[:].unsqueeze(2).to_broadcast([P, 24, NG]),
+                in1=gmask[:].unsqueeze(1).to_broadcast([P, 24, NG]),
                 op=ALU.mult,
             )
 
@@ -275,13 +277,13 @@ def tile_kanlinear_t_kernel(tc, x, coefficients, out):
                 )
 
         def powers_scalar(duo):
-            ph = work.tile([P, 16, 32, 4], F32, tag="ph")
-            pw = work.tile([P, 16, 4, 4], F32, tag="pw")
+            ph = work.tile([P, NG, NPW, NG], F32, tag="ph")
+            pw = work.tile([P, NG, 3, NG], F32, tag="pw")
             hv = pair_view(hh, duo * W2)
             nc.scalar.activation(out=ph[:, :, 0, :], in_=hv, func=ACT.Identity, scale=0.0, bias=1.0)
             nc.scalar.copy(out=ph[:, :, 1, :], in_=hv)
             nc.scalar.activation(out=pw[:, :, 0, :], in_=hv, func=ACT.Square)
-            for lv in range(1, 4):
+            for lv in range(1, 3):
                 nc.scalar.activation(out=pw[:, :, lv, :], in_=pw[:, :, lv - 1, :], func=ACT.Square)
             return (ph, pw)
 
@@ -291,33 +293,29 @@ def tile_kanlinear_t_kernel(tc, x, coefficients, out):
             nc.vector.tensor_tensor(
                 out=ph[:, :, n : 2 * n, :],
                 in0=ph[:, :, 0:n, :],
-                in1=pw[:, :, lv, :].unsqueeze(2).to_broadcast([P, 16, n, 4]),
+                in1=pw[:, :, lv, :].unsqueeze(2).to_broadcast([P, NG, n, NG]),
                 op=ALU.mult,
             )
 
-        def pieces_a(ph, q):
+        def pieces_a(ph, hq):
             ft = psum.tile([P, 4, P], F32, tag="ft")
             for s in range(4):
-                nc.tensor.transpose(out=ft[:, s, :], in_=ph[:, q * 4 + s, :, :].rearrange("q p g -> q (p g)"), identity=ident_f[:])
+                nc.tensor.transpose(out=ft[:, s, :], in_=ph[:, hq * 4 + s, :, :].rearrange("q p g -> q (p g)"), identity=ident_f[:])
             fts = work.tile([P, 4, P], F32, tag="fts")
             nc.scalar.copy(out=fts[:], in_=ft[:])
             return fts
 
-        def pieces_b(fts):
+        def pieces_b(fts, j):
             pa = psum.tile([P, 512], F32, tag="pa")
-            for s in range(4):
-                nc.tensor.matmul(out=pa[:, s * 96 : (s + 1) * 96], lhsT=fts[:, s, :], rhs=wmat[:].rearrange("q e g -> q (e g)"), start=True, stop=True)
+            for s in range(2):
+                nc.tensor.matmul(out=pa[:, s * 192 : (s + 1) * 192], lhsT=fts[:, 2 * j + s, :], rhs=wmat[:].rearrange("q e g -> q (e g)"), start=True, stop=True)
             return pa
 
         def pieces_c(at, pa, q):
             nc.scalar.copy(
-                out=at[:, 4:28, q * 16 : (q + 1) * 16].rearrange("q e (s g) -> q e s g", g=4),
-                in_=pa[:, 0:384].rearrange("q (s e g) -> q e s g", s=4, e=24, g=4),
+                out=at[:, :, q * 16 : (q + 1) * 16].rearrange("q e (s g) -> q e s g", g=NG),
+                in_=pa[:, 0:384].rearrange("q (s e g) -> q e s g", s=2, e=24, g=NG),
             )
-
-        def pieces_outer(at, duo):
-            nc.scalar.copy(out=at[:, 0:4, :], in_=xe[:, 0:4, duo * W2 : (duo + 1) * W2])
-            nc.scalar.copy(out=at[:, 28:32, :], in_=xe[:, 4:8, duo * W2 : (duo + 1) * W2])
 
         def shift_sign(chain, duo, k, src):
             p0 = duo * W2
@@ -326,9 +324,12 @@ def tile_kanlinear_t_kernel(tc, x, coefficients, out):
             gcur = work.tile([P, ROWS, W2], BF16, tag="gs%s" % chain, bufs=1)
             if k == 4:
                 for off, m_pos, m_neg in ((0, ml_pos, ml_neg), (32, mr_pos, mr_neg)):
-                    for row, mm in ((0, m_pos), (16, m_neg)):
-                        grp = (off + row, 16, 1, 0)
-                        nc.vector.tensor_tensor(out=rows_view(gcur, grp, 0), in0=src[:, row : row + 16, :], in1=pair_rows(mm, p0, grp), op=ALU.mult)
+                    for row, mm in ((4, m_pos), (16, m_neg)):
+                        grp = (off + row, 12, 1, 0)
+                        nc.vector.tensor_tensor(out=rows_view(gcur, grp, 0), in0=src[:, row - 4 : row + 8, :], in1=pair_rows(mm, p0, grp), op=ALU.mult)
+                    for row, first, mm in ((0, 0, m_pos), (28, 4, m_neg)):
+                        grp = (off + row, 4, 1, 0)
+                        nc.vector.tensor_tensor(out=rows_view(gcur, grp, 0), in0=xe[:, first : first + 4, p0 : p0 + W2], in1=pair_rows(mm, p0, grp), op=ALU.mult)
             else:
                 for want, mu in ((1, mu_pos[k]), (-1, mu_neg[k])):
                     for grp in row_groups(out_lo - a, 64, lambda e: chi(k + 1, e) * chi(k, e), want):
@@ -361,9 +362,12 @@ def tile_kanlinear_t_kernel(tc, x, coefficients, out):
                     nc.tensor.transpose(out=xt[:, c, tq, :], in_=yc[:, tq, c * 16 : (c + 1) * 16, :].rearrange("q i s -> q (i s)"), identity=ident_b[:])
             return xt
 
-        def turn_c(xt):
+        def turn_c(xt, last):
             grouped = work.tile([P, 2, P, 4], BF16, tag="grouped", align_bytes=64, bufs=4)
-            nc.scalar.copy(out=grouped[:], in_=xt[:].rearrange("q c t r -> q c r t"))
+            if last:
+                nc.vector.tensor_copy(out=grouped[:], in_=xt[:].rearrange("q c t r -> q c r t"))
+            else:
+                nc.scalar.copy(out=grouped[:], in_=xt[:].rearrange("q c t r -> q c r t"))
             return grouped
 
         def quantise(grouped):
@@ -372,7 +376,7 @@ def tile_kanlinear_t_kernel(tc, x, coefficients, out):
             nc.vector.quantize_mx(out=b_codes[:].bitcast(FP8X4), scales=b_scales[:], in_=grouped[:].rearrange("q c r t -> q (c r t)"))
             return (b_codes, b_scales)
 
-        def multiply(t, operand):
+        def multiply(t, operand, last):
             b_codes, b_scales = operand
             res = work.tile([P, NO], F32, tag="res")
             for n in range(2):
@@ -387,19 +391,19 @@ def tile_kanlinear_t_kernel(tc, x, coefficients, out):
                         start=(c == 0),
                         stop=(c == 1),
                     )
-                nc.scalar.copy(out=res[:, n * 512 : (n + 1) * 512], in_=acc[:])
+                if last and n == 1:
+                    nc.vector.tensor_copy(out=res[:, n * 512 : (n + 1) * 512], in_=acc[:])
+                else:
+                    nc.scalar.copy(out=res[:, n * 512 : (n + 1) * 512], in_=acc[:])
             nc.sync.dma_start(out=out_v[t], in_=res[:])
 
-        def pieces(duo, php, chain):
-            at = work.tile([P, 32, W2], BF16, tag="at%s" % chain)
-            fts_next = pieces_a(php[0], 0)
+        def pieces(php, chain):
+            at = work.tile([P, 24, W2], BF16, tag="at%s" % chain)
+            f0 = pieces_a(php[0], 0)
+            f1 = pieces_a(php[0], 1)
             for q in range(4):
-                fts = fts_next
-                if q < 3:
-                    fts_next = pieces_a(php[0], q + 1)
-                pa = pieces_b(fts)
+                pa = pieces_b(f0 if q < 2 else f1, q % 2)
                 pieces_c(at, pa, q)
-            pieces_outer(at, duo)
             return at
 
         ex = ctx.enter_context(tc.tile_pool(name="ex", bufs=1))
@@ -438,17 +442,17 @@ def tile_kanlinear_t_kernel(tc, x, coefficients, out):
         php_a = powers_scalar(0)
         php_b = powers_scalar(1)
         taylor_matrix()
-        for lv in range(4):
+        for lv in range(3):
             powers_step(php_a, lv)
             powers_step(php_b, lv)
         qq_cur = outer_logs(0)
         outer_scalar(qq_cur, 0)
         outer_vector(qq_cur, 0)
-        at_a = pieces(0, php_a, "a")
+        at_a = pieces(php_a, "a")
         php_a = powers_scalar(2)
-        for lv in range(4):
+        for lv in range(3):
             powers_step(php_a, lv)
-        at_b = pieces(1, php_b, "b")
+        at_b = pieces(php_b, "b")
         php_b = powers_scalar(3)
 
         fin_a = None
@@ -458,6 +462,7 @@ def tile_kanlinear_t_kernel(tc, x, coefficients, out):
             finishing = m >= 1
             preparing = m + 1 < NQ
             ahead = m + 2 < NQ
+            last = m == NQ
             da = 2 * m
             db = 2 * m + 1
             t0 = 4 * (m - 1)
@@ -468,16 +473,15 @@ def tile_kanlinear_t_kernel(tc, x, coefficients, out):
             if finishing:
                 yc0 = turn_a(fin_a, 0)
             if preparing:
-                at_a = work.tile([P, 32, W2], BF16, tag="ata")
+                at_a = work.tile([P, 24, W2], BF16, tag="ata")
                 f0 = pieces_a(php_a[0], 0)
             if finishing:
                 yc1 = turn_a(fin_a, 1)
                 xt0 = turn_b(yc0)
             if preparing:
-                f1 = pieces_a(php_a[0], 1)
-                p0 = pieces_b(f0)
+                p0 = pieces_b(f0, 0)
             if finishing:
-                grouped0 = turn_c(xt0)
+                grouped0 = turn_c(xt0, last)
             if shifting:
                 ga = shift_sign("a", da, 4, old_a)
                 gb = shift_sign("b", db, 4, old_b)
@@ -497,14 +501,14 @@ def tile_kanlinear_t_kernel(tc, x, coefficients, out):
             if finishing:
                 xt1 = turn_b(yc1)
             if preparing:
-                p1 = pieces_b(f1)
+                p1 = pieces_b(f0, 1)
             if finishing:
                 yc2 = turn_a(fin_b, 0)
             if preparing:
-                f2 = pieces_a(php_a[0], 2)
+                f1 = pieces_a(php_a[0], 1)
             if finishing:
-                grouped1 = turn_c(xt1)
-                multiply(t0, op0)
+                grouped1 = turn_c(xt1, last)
+                multiply(t0, op0, last)
             if preparing:
                 pieces_c(at_a, p1, 1)
             if shifting:
@@ -517,30 +521,24 @@ def tile_kanlinear_t_kernel(tc, x, coefficients, out):
             if shifting:
                 ya = shift_pick("a", 3, ga)
                 yb = shift_pick("b", 3, gb)
-            if preparing:
-                powers_step(php_b, 3)
             if finishing:
                 xt2 = turn_b(yc2)
             if preparing:
-                p2 = pieces_b(f2)
+                p2 = pieces_b(f1, 0)
             if finishing:
                 yc3 = turn_a(fin_b, 1)
-            if preparing:
-                f3 = pieces_a(php_a[0], 3)
-            if finishing:
-                grouped2 = turn_c(xt2)
+                grouped2 = turn_c(xt2, last)
             if preparing:
                 pieces_c(at_a, p2, 2)
             if finishing:
-                multiply(t0 + 1, op1)
+                multiply(t0 + 1, op1, last)
                 xt3 = turn_b(yc3)
             if preparing:
-                p3 = pieces_b(f3)
+                p3 = pieces_b(f1, 1)
             if finishing:
-                grouped3 = turn_c(xt3)
+                grouped3 = turn_c(xt3, last)
             if preparing:
                 pieces_c(at_a, p3, 3)
-                pieces_outer(at_a, da + 2)
             if ahead:
                 php_a = powers_scalar(da + 4)
             if shifting:
@@ -556,26 +554,23 @@ def tile_kanlinear_t_kernel(tc, x, coefficients, out):
             if m == 0 or m == 2 or m == 3:
                 outer_vector(qq_cur, 1 if m == 0 else m)
             if preparing:
-                at_b = work.tile([P, 32, W2], BF16, tag="atb")
+                at_b = work.tile([P, 24, W2], BF16, tag="atb")
                 f0 = pieces_a(php_b[0], 0)
                 f1 = pieces_a(php_b[0], 1)
-                p0 = pieces_b(f0)
+                p0 = pieces_b(f0, 0)
             if finishing:
-                multiply(t0 + 2, op2)
+                multiply(t0 + 2, op2, last)
             if preparing:
                 pieces_c(at_b, p0, 0)
-                p1 = pieces_b(f1)
-                f2 = pieces_a(php_b[0], 2)
+                p1 = pieces_b(f0, 1)
                 pieces_c(at_b, p1, 1)
             if finishing:
-                multiply(t0 + 3, op3)
+                multiply(t0 + 3, op3, last)
             if preparing:
-                p2 = pieces_b(f2)
-                f3 = pieces_a(php_b[0], 3)
+                p2 = pieces_b(f1, 0)
                 pieces_c(at_b, p2, 2)
-                p3 = pieces_b(f3)
+                p3 = pieces_b(f1, 1)
                 pieces_c(at_b, p3, 3)
-                pieces_outer(at_b, db + 2)
             if ahead:
                 php_b = powers_scalar(db + 4)
             if m == 0:
@@ -584,16 +579,21 @@ def tile_kanlinear_t_kernel(tc, x, coefficients, out):
                     weights_block(a)
             if m == 1 or m == 2:
                 outer_scalar(qq_cur, m + 1)
-            for k in (1, 0):
-                if shifting:
-                    ga = shift_sign("a", da, k, ya)
-                    gb = shift_sign("b", db, k, yb)
-                if ahead:
-                    powers_step(php_a, 2 - 2 * k)
-                if shifting:
-                    ya = shift_pick("a", k, ga)
-                    yb = shift_pick("b", k, gb)
-                if ahead:
-                    powers_step(php_a, 3 - 2 * k)
-            fin_a = ya
-            fin_b = yb
+            if shifting:
+                ga = shift_sign("a", da, 1, ya)
+                gb = shift_sign("b", db, 1, yb)
+            if ahead:
+                powers_step(php_a, 0)
+            if shifting:
+                ya = shift_pick("a", 1, ga)
+                yb = shift_pick("b", 1, gb)
+            if ahead:
+                powers_step(php_a, 1)
+            if shifting:
+                ga = shift_sign("a", da, 0, ya)
+                gb = shift_sign("b", db, 0, yb)
+            if ahead:
+                powers_step(php_a, 2)
+            if shifting:
+                fin_a = shift_pick("a", 0, ga)
+                fin_b = shift_pick("b", 0, gb)

@@ -24,7 +24,7 @@ NP = NT * NI
 ND = NT // 2
 NQ = ND // 2
 W2 = 2 * NI
-ROWS = 80
+ROWS = 48
 UMAX = 62.99999
 NPW = 16
 NG = P // NPW
@@ -148,10 +148,8 @@ def tile_kanlinear_t_kernel(tc, x, coefficients, out):
         for k in range(5):
             mu_pos.append(keep.tile([P, NP], BF16, name="mu_pos%d" % k))
             mu_neg.append(keep.tile([P, NP], BF16, name="mu_neg%d" % k))
-        ml_pos = keep.tile([P, NP], BF16)
-        ml_neg = keep.tile([P, NP], BF16)
-        mr_pos = keep.tile([P, NP], BF16)
-        mr_neg = keep.tile([P, NP], BF16)
+        mn_pos = keep.tile([P, NP], BF16)
+        mn_neg = keep.tile([P, NP], BF16)
         xe = keep.tile([P, 8, NP], BF16)
 
         tb_hi = keep.tile([P, 12, NPW], F32)
@@ -185,49 +183,75 @@ def tile_kanlinear_t_kernel(tc, x, coefficients, out):
             nc.scalar.copy(out=gw[:, :, a * P : (a + 1) * P, :], in_=wt[:].rearrange("q c t r -> q c r t"))
 
         with tc.tile_pool(name="pre", bufs=1) as pre:
+            halves = (slice(0, NP // 2), slice(NP // 2, NP))
             xb = pre.tile([P, NP], BF16)
             nc.sync.dma_start(out=xb[:], in_=x.rearrange("(p t) i -> p (t i)", t=NT))
             th = pre.tile([P, NP], F32, tag="rot", bufs=3)
-            nc.scalar.activation(out=th[:], in_=xb[:], func=ACT.Tanh)
+            for hs in halves:
+                nc.scalar.activation(out=th[:, hs], in_=xb[:, hs], func=ACT.Tanh)
 
             for a in range(4):
                 weights_block(a)
 
             u0 = pre.tile([P, NP], F32, tag="rot", bufs=3)
-            nc.vector.tensor_scalar(out=u0[:], in0=th[:], scalar1=31.5, scalar2=31.5, op0=ALU.mult, op1=ALU.add)
+            for hs in halves:
+                nc.vector.tensor_scalar(out=u0[:, hs], in0=th[:, hs], scalar1=31.5, scalar2=31.5, op0=ALU.mult, op1=ALU.add)
             uu = pre.tile([P, NP], F32)
-            nc.vector.tensor_scalar(out=uu[:], in0=u0[:], scalar1=UMAX, scalar2=0.0, op0=ALU.min, op1=ALU.max)
+            for hs in halves:
+                nc.vector.tensor_scalar(out=uu[:, hs], in0=u0[:, hs], scalar1=UMAX, scalar2=0.0, op0=ALU.min, op1=ALU.max)
             ji = pre.tile([P, NP], I32)
-            nc.vector.tensor_copy(out=ji[:], in_=uu[:])
+            for hs in halves:
+                nc.vector.tensor_copy(out=ji[:, hs], in_=uu[:, hs])
             jf = pre.tile([P, NP], F32, tag="rot", bufs=3)
-            nc.vector.tensor_copy(out=jf[:], in_=ji[:])
+            for hs in halves:
+                nc.vector.tensor_copy(out=jf[:, hs], in_=ji[:, hs])
             fr = pre.tile([P, NP], F32, tag="rot", bufs=3)
-            nc.vector.tensor_tensor(out=fr[:], in0=uu[:], in1=jf[:], op=ALU.subtract)
+            for hs in halves:
+                nc.vector.tensor_tensor(out=fr[:, hs], in0=uu[:, hs], in1=jf[:, hs], op=ALU.subtract)
             j1a = pre.tile([P, NP], F32, tag="rot", bufs=3)
-            nc.vector.scalar_tensor_tensor(out=j1a[:], in0=fr[:], scalar=1.0, in1=jf[:], op0=ALU.is_ge, op1=ALU.add)
+            for hs in halves:
+                nc.vector.scalar_tensor_tensor(out=j1a[:, hs], in0=fr[:, hs], scalar=1.0, in1=jf[:, hs], op0=ALU.is_ge, op1=ALU.add)
             j1b = pre.tile([P, NP], F32, tag="rot", bufs=3)
-            nc.vector.scalar_tensor_tensor(out=j1b[:], in0=fr[:], scalar=0.0, in1=j1a[:], op0=ALU.is_ge, op1=ALU.add)
+            for hs in halves:
+                nc.vector.scalar_tensor_tensor(out=j1b[:, hs], in0=fr[:, hs], scalar=0.0, in1=j1a[:, hs], op0=ALU.is_ge, op1=ALU.add)
             j1i = pre.tile([P, NP], I32)
-            nc.vector.tensor_copy(out=j1i[:], in_=j1b[:])
+            for hs in halves:
+                nc.vector.tensor_copy(out=j1i[:, hs], in_=j1b[:, hs])
             j1 = pre.tile([P, NP], F32, tag="rot", bufs=3)
-            nc.vector.tensor_copy(out=j1[:], in_=j1i[:])
+            for hs in halves:
+                nc.vector.tensor_copy(out=j1[:, hs], in_=j1i[:, hs])
             hm = pre.tile([P, NP], F32, tag="rot", bufs=3)
-            nc.vector.tensor_tensor(out=hm[:], in0=uu[:], in1=j1[:], op=ALU.subtract)
-            nc.vector.tensor_scalar_add(out=hh[:], in0=hm[:], scalar1=0.5)
-
-            bit5 = pre.tile([P, NP], I32, tag="bit", bufs=2)
-            nc.vector.tensor_scalar(out=bit5[:], in0=j1i[:], scalar1=5, scalar2=1, op0=ALU.logical_shift_right, op1=ALU.bitwise_and)
-            b5 = pre.tile([P, NP], BF16)
-            nc.vector.tensor_copy(out=b5[:], in_=bit5[:])
+            for hs in halves:
+                nc.vector.tensor_tensor(out=hm[:, hs], in0=uu[:, hs], in1=j1[:, hs], op=ALU.subtract)
+            h0 = pre.tile([P, NP], F32, tag="rot", bufs=3)
+            for hs in halves:
+                nc.vector.tensor_scalar_add(out=h0[:, hs], in0=hm[:, hs], scalar1=0.5)
+            dj = pre.tile([P, NP], F32)
+            for hs in halves:
+                nc.vector.tensor_scalar_add(out=dj[:, hs], in0=j1[:, hs], scalar1=-32.0)
+            s05 = pre.tile([P, NP], F32)
+            for hs in halves:
+                nc.vector.tensor_scalar(out=s05[:, hs], in0=dj[:, hs], scalar1=0.0, scalar2=0.5, op0=ALU.is_ge, op1=ALU.subtract)
+            for hs in halves:
+                nc.vector.scalar_tensor_tensor(out=hh[:, hs], in0=h0[:, hs], scalar=2.0, in1=s05[:, hs], op0=ALU.mult, op1=ALU.mult)
+            rr = pre.tile([P, NP], F32, tag="rot", bufs=3)
+            for hs in halves:
+                nc.vector.scalar_tensor_tensor(out=rr[:, hs], in0=dj[:, hs], scalar=2.0, in1=s05[:, hs], op0=ALU.mult, op1=ALU.mult)
+            ri = pre.tile([P, NP], I32)
+            for hs in halves:
+                nc.vector.tensor_copy(out=ri[:, hs], in_=rr[:, hs])
+            nc.vector.tensor_scalar_mul(out=mn_pos[:], in0=s05[:], scalar1=2.0)
+            bit_prev = None
             for k in (4, 3, 2, 1, 0):
-                bit = pre.tile([P, NP], I32, tag="bit", bufs=2)
-                nc.vector.tensor_scalar(out=bit[:], in0=j1i[:], scalar1=k, scalar2=1, op0=ALU.logical_shift_right, op1=ALU.bitwise_and)
-                nc.vector.tensor_scalar(out=mu_pos[k][:], in0=bit[:], scalar1=-2.0, scalar2=1.0, op0=ALU.mult, op1=ALU.add)
-                nc.vector.tensor_scalar(out=mu_neg[k][:], in0=bit[:], scalar1=2.0, scalar2=-1.0, op0=ALU.mult, op1=ALU.add)
-            nc.vector.tensor_tensor(out=mr_pos[:], in0=mu_pos[4][:], in1=b5[:], op=ALU.mult)
-            nc.vector.tensor_tensor(out=ml_pos[:], in0=mu_pos[4][:], in1=mr_pos[:], op=ALU.subtract)
-            nc.vector.tensor_scalar_mul(out=mr_neg[:], in0=mr_pos[:], scalar1=-1.0)
-            nc.vector.tensor_scalar_mul(out=ml_neg[:], in0=ml_pos[:], scalar1=-1.0)
+                bit = pre.tile([P, NP], I32, tag="bit", bufs=3)
+                nc.vector.tensor_scalar(out=bit[:], in0=ri[:], scalar1=k, scalar2=1, op0=ALU.logical_shift_right, op1=ALU.bitwise_and)
+                if k < 4:
+                    nc.vector.tensor_scalar(out=mu_pos[k + 1][:], in0=bit_prev[:], scalar1=-2.0, scalar2=1.0, op0=ALU.mult, op1=ALU.add)
+                bit_prev = bit
+            nc.vector.tensor_scalar(out=mu_pos[0][:], in0=bit_prev[:], scalar1=-2.0, scalar2=1.0, op0=ALU.mult, op1=ALU.add)
+            for k in (4, 3, 2, 1, 0):
+                nc.gpsimd.tensor_scalar(out=mu_neg[k][:], in0=mu_pos[k][:], scalar1=-1.0, scalar2=0.0, op0=ALU.mult, op1=ALU.add)
+            nc.gpsimd.tensor_scalar(out=mn_neg[:], in0=mn_pos[:], scalar1=-1.0, scalar2=0.0, op0=ALU.mult, op1=ALU.add)
 
         work = ctx.enter_context(tc.tile_pool(name="work", bufs=2))
 
@@ -313,42 +337,43 @@ def tile_kanlinear_t_kernel(tc, x, coefficients, out):
 
         def pieces_c(at, pa, q):
             nc.scalar.copy(
-                out=at[:, :, q * 16 : (q + 1) * 16].rearrange("q e (s g) -> q e s g", g=NG),
+                out=at[:, 4:28, q * 16 : (q + 1) * 16].rearrange("q e (s g) -> q e s g", g=NG),
                 in_=pa[:, 0:384].rearrange("q (s e g) -> q e s g", s=2, e=24, g=NG),
             )
 
-        def shift_sign(chain, duo, k, src):
-            p0 = duo * W2
-            a = 1 << k
-            out_lo = 32 - a if k > 0 else 32
+        def pieces_outer(at, duo):
+            nc.scalar.copy(out=at[:, 0:4, :], in_=xe[:, 0:4, duo * W2 : (duo + 1) * W2])
+            nc.scalar.copy(out=at[:, 28:32, :], in_=xe[:, 4:8, duo * W2 : (duo + 1) * W2])
+
+        def signed(chain, duo, src, pattern, m_pos, m_neg):
             gcur = work.tile([P, ROWS, W2], BF16, tag="gs%s" % chain, bufs=1)
-            if k == 4:
-                for off, m_pos, m_neg in ((0, ml_pos, ml_neg), (32, mr_pos, mr_neg)):
-                    for row, mm in ((4, m_pos), (16, m_neg)):
-                        grp = (off + row, 12, 1, 0)
-                        nc.vector.tensor_tensor(out=rows_view(gcur, grp, 0), in0=src[:, row - 4 : row + 8, :], in1=pair_rows(mm, p0, grp), op=ALU.mult)
-                    for row, first, mm in ((0, 0, m_pos), (28, 4, m_neg)):
-                        grp = (off + row, 4, 1, 0)
-                        nc.vector.tensor_tensor(out=rows_view(gcur, grp, 0), in0=xe[:, first : first + 4, p0 : p0 + W2], in1=pair_rows(mm, p0, grp), op=ALU.mult)
-            else:
-                for want, mu in ((1, mu_pos[k]), (-1, mu_neg[k])):
-                    for grp in row_groups(out_lo - a, 64, lambda e: chi(k + 1, e) * chi(k, e), want):
-                        nc.vector.tensor_tensor(out=rows_view(gcur, grp, 0), in0=rows_view(src, grp, 0), in1=pair_rows(mu, p0, grp), op=ALU.mult)
+            for want, mm in ((1, m_pos), (-1, m_neg)):
+                for grp in row_groups(0, 32, pattern, want):
+                    nc.vector.tensor_tensor(out=rows_view(gcur, grp, 0), in0=rows_view(src, grp, 0), in1=pair_rows(mm, duo * W2, grp), op=ALU.mult)
             return gcur
+
+        def shift_sign(chain, duo, k, src):
+            if k == 4:
+                return signed(chain, duo, src, lambda e: chi(4, e), mu_pos[4], mu_neg[4])
+            return signed(chain, duo, src, lambda e: chi(k + 1, e) * chi(k, e), mu_pos[k], mu_neg[k])
 
         def shift_pick(chain, k, gcur):
             a = 1 << k
-            out_lo = 32 - a if k > 0 else 32
-            if k > 0:
-                ycur = work.tile([P, ROWS, W2], BF16, tag="ys%s" % chain, bufs=1)
-                base = 0
-            else:
-                ycur = work.tile([P, 34, W2], BF16, tag="yfin%s" % chain)
-                base = 32
+            ycur = work.tile([P, ROWS, W2], BF16, tag="ys%s" % chain, bufs=1)
+            nc.vector.tensor_scalar_max(out=ycur[:, 0:a, :], in0=gcur[:, 0:a, :], scalar1=0.0)
             for want, op in ((1, ALU.max), (-1, ALU.min)):
-                for grp in row_groups(out_lo, 64, lambda e: chi(k, e), want):
-                    nc.vector.tensor_tensor(out=rows_view(ycur, grp, base), in0=rows_view(gcur, grp, 0), in1=rows_view(gcur, grp, a), op=op)
+                for grp in row_groups(a, 32, lambda e: chi(k, e), want):
+                    nc.vector.tensor_tensor(out=rows_view(ycur, grp, 0), in0=rows_view(gcur, grp, 0), in1=rows_view(gcur, grp, a), op=op)
             return ycur
+
+        def flip_sign(chain, duo, src):
+            return signed(chain, duo, src, lambda e: chi(0, e) * chi(4, e), mn_pos, mn_neg)
+
+        def flip_pick(chain, gcur):
+            yfin = work.tile([P, 32, W2], BF16, tag="yfin%s" % chain)
+            nc.vector.tensor_tensor(out=yfin[:, 0:16, :], in0=gcur[:, 0:16, :], in1=gcur[:, 31:15:-1, :], op=ALU.max)
+            nc.vector.tensor_tensor(out=yfin[:, 16:32, :], in0=gcur[:, 16:32, :], in1=gcur[:, 15::-1, :], op=ALU.min)
+            return yfin
 
         def turn_a(yfin, a):
             yc = work.tile([P, 4, NI, 8], BF16, tag="yc")
@@ -397,13 +422,14 @@ def tile_kanlinear_t_kernel(tc, x, coefficients, out):
                     nc.scalar.copy(out=res[:, n * 512 : (n + 1) * 512], in_=acc[:])
             nc.sync.dma_start(out=out_v[t], in_=res[:])
 
-        def pieces(php, chain):
-            at = work.tile([P, 24, W2], BF16, tag="at%s" % chain)
+        def pieces(duo, php, chain):
+            at = work.tile([P, 32, W2], BF16, tag="at%s" % chain)
             f0 = pieces_a(php[0], 0)
             f1 = pieces_a(php[0], 1)
             for q in range(4):
                 pa = pieces_b(f0 if q < 2 else f1, q % 2)
                 pieces_c(at, pa, q)
+            pieces_outer(at, duo)
             return at
 
         ex = ctx.enter_context(tc.tile_pool(name="ex", bufs=1))
@@ -448,11 +474,11 @@ def tile_kanlinear_t_kernel(tc, x, coefficients, out):
         qq_cur = outer_logs(0)
         outer_scalar(qq_cur, 0)
         outer_vector(qq_cur, 0)
-        at_a = pieces(php_a, "a")
+        at_a = pieces(0, php_a, "a")
         php_a = powers_scalar(2)
         for lv in range(3):
             powers_step(php_a, lv)
-        at_b = pieces(php_b, "b")
+        at_b = pieces(1, php_b, "b")
         php_b = powers_scalar(3)
 
         fin_a = None
@@ -473,7 +499,7 @@ def tile_kanlinear_t_kernel(tc, x, coefficients, out):
             if finishing:
                 yc0 = turn_a(fin_a, 0)
             if preparing:
-                at_a = work.tile([P, 24, W2], BF16, tag="ata")
+                at_a = work.tile([P, 32, W2], BF16, tag="ata")
                 f0 = pieces_a(php_a[0], 0)
             if finishing:
                 yc1 = turn_a(fin_a, 1)
@@ -539,6 +565,7 @@ def tile_kanlinear_t_kernel(tc, x, coefficients, out):
                 grouped3 = turn_c(xt3, last)
             if preparing:
                 pieces_c(at_a, p3, 3)
+                pieces_outer(at_a, da + 2)
             if ahead:
                 php_a = powers_scalar(da + 4)
             if shifting:
@@ -554,7 +581,7 @@ def tile_kanlinear_t_kernel(tc, x, coefficients, out):
             if m == 0 or m == 2 or m == 3:
                 outer_vector(qq_cur, 1 if m == 0 else m)
             if preparing:
-                at_b = work.tile([P, 24, W2], BF16, tag="atb")
+                at_b = work.tile([P, 32, W2], BF16, tag="atb")
                 f0 = pieces_a(php_b[0], 0)
                 f1 = pieces_a(php_b[0], 1)
                 p0 = pieces_b(f0, 0)
@@ -571,6 +598,7 @@ def tile_kanlinear_t_kernel(tc, x, coefficients, out):
                 pieces_c(at_b, p2, 2)
                 p3 = pieces_b(f1, 1)
                 pieces_c(at_b, p3, 3)
+                pieces_outer(at_b, db + 2)
             if ahead:
                 php_b = powers_scalar(db + 4)
             if m == 0:
@@ -595,5 +623,9 @@ def tile_kanlinear_t_kernel(tc, x, coefficients, out):
             if ahead:
                 powers_step(php_a, 2)
             if shifting:
-                fin_a = shift_pick("a", 0, ga)
-                fin_b = shift_pick("b", 0, gb)
+                ya = shift_pick("a", 0, ga)
+                yb = shift_pick("b", 0, gb)
+                ga = flip_sign("a", da, ya)
+                gb = flip_sign("b", db, yb)
+                fin_a = flip_pick("a", ga)
+                fin_b = flip_pick("b", gb)

@@ -24,7 +24,7 @@ NP = NT * NI
 ND = NT // 2
 NQ = ND // 2
 W2 = 2 * NI
-ROWS = 48
+ROWS = 64
 UMAX = 62.99999
 NPW = 16
 NG = P // NPW
@@ -87,22 +87,23 @@ def row_groups(lo, hi, sign_of, want):
         else:
             e += 1
     groups = []
-    n = 0
-    while n < len(runs):
-        s, ln = runs[n]
-        cnt = 1
-        per = 0
-        while n + cnt < len(runs) and runs[n + cnt][1] == ln:
-            step = runs[n + cnt][0] - runs[n + cnt - 1][0]
-            if cnt == 1:
-                per = step
-            if step != per:
-                break
-            cnt += 1
-        if cnt == 1:
+    for ln in sorted(set([r[1] for r in runs])):
+        starts = [r[0] for r in runs if r[1] == ln]
+        n = 0
+        while n < len(starts):
+            cnt = 1
             per = 0
-        groups.append((s, ln, cnt, per))
-        n += cnt
+            while n + cnt < len(starts):
+                step = starts[n + cnt] - starts[n + cnt - 1]
+                if cnt == 1:
+                    per = step
+                if step != per:
+                    break
+                cnt += 1
+            if cnt == 1:
+                per = 0
+            groups.append((starts[n], ln, cnt, per))
+            n += cnt
     return groups
 
 
@@ -143,13 +144,14 @@ def tile_kanlinear_t_kernel(tc, x, coefficients, out):
         w_codes = keep.tile([P, 2, NO], U32, align_bytes=64)
         w_scales = keep.tile([P, 2, NO], U8, align_bytes=64)
         hh = keep.tile([P, NP], F32)
+        sg = keep.tile([P, NP], F32)
+        sgh = keep.tile([P, NP], F32)
         mu_pos = []
         mu_neg = []
         for k in range(5):
             mu_pos.append(keep.tile([P, NP], BF16, name="mu_pos%d" % k))
             mu_neg.append(keep.tile([P, NP], BF16, name="mu_neg%d" % k))
         mn_pos = keep.tile([P, NP], BF16)
-        mn_neg = keep.tile([P, NP], BF16)
         xe = keep.tile([P, 8, NP], BF16)
 
         tb_hi = keep.tile([P, 12, NPW], F32)
@@ -245,13 +247,14 @@ def tile_kanlinear_t_kernel(tc, x, coefficients, out):
             for k in (4, 3, 2, 1, 0):
                 bit = pre.tile([P, NP], I32, tag="bit", bufs=3)
                 nc.vector.tensor_scalar(out=bit[:], in0=ri[:], scalar1=k, scalar2=1, op0=ALU.logical_shift_right, op1=ALU.bitwise_and)
+                if k == 3:
+                    nc.vector.tensor_scalar(out=sg[:], in0=bit_prev[:], scalar1=-2.0, scalar2=1.0, op0=ALU.mult, op1=ALU.add)
                 if k < 4:
                     nc.vector.tensor_scalar(out=mu_pos[k + 1][:], in0=bit_prev[:], scalar1=-2.0, scalar2=1.0, op0=ALU.mult, op1=ALU.add)
+                if k == 2:
+                    nc.vector.tensor_tensor(out=sgh[:], in0=sg[:], in1=hh[:], op=ALU.mult)
                 bit_prev = bit
             nc.vector.tensor_scalar(out=mu_pos[0][:], in0=bit_prev[:], scalar1=-2.0, scalar2=1.0, op0=ALU.mult, op1=ALU.add)
-            for k in (4, 3, 2, 1, 0):
-                nc.gpsimd.tensor_scalar(out=mu_neg[k][:], in0=mu_pos[k][:], scalar1=-1.0, scalar2=0.0, op0=ALU.mult, op1=ALU.add)
-            nc.gpsimd.tensor_scalar(out=mn_neg[:], in0=mn_pos[:], scalar1=-1.0, scalar2=0.0, op0=ALU.mult, op1=ALU.add)
 
         work = ctx.enter_context(tc.tile_pool(name="work", bufs=2))
 
@@ -284,7 +287,7 @@ def tile_kanlinear_t_kernel(tc, x, coefficients, out):
             wc = wp.tile([P, 24], F32, bufs=1)
             nc.vector.tensor_scalar(out=wc[:, 0:12], in0=w0[:], scalar1=sgnp[:, 0:1], scalar2=None, op0=ALU.mult)
             for e in range(16, 28):
-                nc.vector.tensor_copy(out=wc[:, e - 4 : e - 3], in_=w0[:, 27 - e : 28 - e])
+                nc.vector.tensor_scalar_mul(out=wc[:, e - 4 : e - 3], in0=w0[:, 27 - e : 28 - e], scalar1=-1.0)
             nc.vector.tensor_tensor(
                 out=wmat[:],
                 in0=wc[:].unsqueeze(2).to_broadcast([P, 24, NG]),
@@ -300,15 +303,15 @@ def tile_kanlinear_t_kernel(tc, x, coefficients, out):
                     in_=gw[:, c, :, :].rearrange("q o t -> q (o t)"),
                 )
 
-        def powers_scalar(duo):
+        def powers_start(duo):
             ph = work.tile([P, NG, NPW, NG], F32, tag="ph")
             pw = work.tile([P, NG, 3, NG], F32, tag="pw")
             hv = pair_view(hh, duo * W2)
-            nc.scalar.activation(out=ph[:, :, 0, :], in_=hv, func=ACT.Identity, scale=0.0, bias=1.0)
-            nc.scalar.copy(out=ph[:, :, 1, :], in_=hv)
-            nc.scalar.activation(out=pw[:, :, 0, :], in_=hv, func=ACT.Square)
+            nc.gpsimd.tensor_copy(out=ph[:, :, 0, :], in_=pair_view(sg, duo * W2))
+            nc.gpsimd.tensor_tensor(out=pw[:, :, 0, :], in0=hv, in1=hv, op=ALU.mult)
+            nc.gpsimd.tensor_copy(out=ph[:, :, 1, :], in_=pair_view(sgh, duo * W2))
             for lv in range(1, 3):
-                nc.scalar.activation(out=pw[:, :, lv, :], in_=pw[:, :, lv - 1, :], func=ACT.Square)
+                nc.gpsimd.tensor_tensor(out=pw[:, :, lv, :], in0=pw[:, :, lv - 1, :], in1=pw[:, :, lv - 1, :], op=ALU.mult)
             return (ph, pw)
 
         def powers_step(php, lv):
@@ -337,13 +340,9 @@ def tile_kanlinear_t_kernel(tc, x, coefficients, out):
 
         def pieces_c(at, pa, q):
             nc.scalar.copy(
-                out=at[:, 4:28, q * 16 : (q + 1) * 16].rearrange("q e (s g) -> q e s g", g=NG),
+                out=at[:, :, q * 16 : (q + 1) * 16].rearrange("q e (s g) -> q e s g", g=NG),
                 in_=pa[:, 0:384].rearrange("q (s e g) -> q e s g", s=2, e=24, g=NG),
             )
-
-        def pieces_outer(at, duo):
-            nc.scalar.copy(out=at[:, 0:4, :], in_=xe[:, 0:4, duo * W2 : (duo + 1) * W2])
-            nc.scalar.copy(out=at[:, 28:32, :], in_=xe[:, 4:8, duo * W2 : (duo + 1) * W2])
 
         def signed(chain, duo, src, pattern, m_pos, m_neg):
             gcur = work.tile([P, ROWS, W2], BF16, tag="gs%s" % chain, bufs=1)
@@ -353,8 +352,6 @@ def tile_kanlinear_t_kernel(tc, x, coefficients, out):
             return gcur
 
         def shift_sign(chain, duo, k, src):
-            if k == 4:
-                return signed(chain, duo, src, lambda e: chi(4, e), mu_pos[4], mu_neg[4])
             return signed(chain, duo, src, lambda e: chi(k + 1, e) * chi(k, e), mu_pos[k], mu_neg[k])
 
         def shift_pick(chain, k, gcur):
@@ -366,18 +363,35 @@ def tile_kanlinear_t_kernel(tc, x, coefficients, out):
                     nc.vector.tensor_tensor(out=rows_view(ycur, grp, 0), in0=rows_view(gcur, grp, 0), in1=rows_view(gcur, grp, a), op=op)
             return ycur
 
+        def first_pick(chain, duo, at):
+            lo = xe[:, 0:4, duo * W2 : (duo + 1) * W2]
+            hi = xe[:, 4:8, duo * W2 : (duo + 1) * W2]
+            ycur = work.tile([P, ROWS, W2], BF16, tag="ys%s" % chain, bufs=1)
+            nc.vector.tensor_scalar_max(out=ycur[:, 0:4, :], in0=lo, scalar1=0.0)
+            nc.vector.tensor_scalar_max(out=ycur[:, 4:16, :], in0=at[:, 0:12, :], scalar1=0.0)
+            nc.vector.tensor_tensor(out=ycur[:, 16:20, :], in0=at[:, 12:16, :], in1=lo, op=ALU.min)
+            nc.vector.tensor_tensor(out=ycur[:, 20:28, :], in0=at[:, 16:24, :], in1=at[:, 0:8, :], op=ALU.min)
+            nc.vector.tensor_tensor(out=ycur[:, 28:32, :], in0=hi, in1=at[:, 8:12, :], op=ALU.min)
+            return ycur
+
         def flip_sign(chain, duo, src):
-            return signed(chain, duo, src, lambda e: chi(0, e) * chi(4, e), mn_pos, mn_neg)
+            gcur = work.tile([P, ROWS, W2], BF16, tag="gs%s" % chain, bufs=1)
+            grp = (0, 32, 1, 0)
+            nc.vector.tensor_tensor(out=rows_view(gcur, grp, 0), in0=rows_view(src, grp, 0), in1=pair_rows(mn_pos, duo * W2, grp), op=ALU.mult)
+            return gcur
 
         def flip_pick(chain, gcur):
             yfin = work.tile([P, 32, W2], BF16, tag="yfin%s" % chain)
-            nc.vector.tensor_tensor(out=yfin[:, 0:16, :], in0=gcur[:, 0:16, :], in1=gcur[:, 31:15:-1, :], op=ALU.max)
-            nc.vector.tensor_tensor(out=yfin[:, 16:32, :], in0=gcur[:, 16:32, :], in1=gcur[:, 15::-1, :], op=ALU.min)
+            nc.vector.tensor_tensor(out=yfin[:, 0:32:2, :], in0=gcur[:, 0:32:2, :], in1=gcur[:, 31::-2, :], op=ALU.max)
+            nc.vector.tensor_tensor(out=yfin[:, 1:32:2, :], in0=gcur[:, 1:32:2, :], in1=gcur[:, 30::-2, :], op=ALU.min)
             return yfin
 
-        def turn_a(yfin, a):
+        def turn_a(yfin, a, swap):
             yc = work.tile([P, 4, NI, 8], BF16, tag="yc")
-            nc.scalar.activation(out=yc[:], in_=yfin[:, 0:32, a * NI : (a + 1) * NI].rearrange("q (t s) i -> q t i s", s=8), func=ACT.Abs)
+            if swap:
+                nc.vector.tensor_copy(out=yc[:], in_=yfin[:, 0:32, a * NI : (a + 1) * NI].rearrange("q (t s) i -> q t i s", s=8))
+            else:
+                nc.scalar.activation(out=yc[:], in_=yfin[:, 0:32, a * NI : (a + 1) * NI].rearrange("q (t s) i -> q t i s", s=8), func=ACT.Abs)
             return yc
 
         def turn_b(yc):
@@ -387,9 +401,11 @@ def tile_kanlinear_t_kernel(tc, x, coefficients, out):
                     nc.tensor.transpose(out=xt[:, c, tq, :], in_=yc[:, tq, c * 16 : (c + 1) * 16, :].rearrange("q i s -> q (i s)"), identity=ident_b[:])
             return xt
 
-        def turn_c(xt, last):
+        def turn_c(xt, last, swap):
             grouped = work.tile([P, 2, P, 4], BF16, tag="grouped", align_bytes=64, bufs=4)
-            if last:
+            if swap:
+                nc.scalar.activation(out=grouped[:], in_=xt[:].rearrange("q c t r -> q c r t"), func=ACT.Abs)
+            elif last:
                 nc.vector.tensor_copy(out=grouped[:], in_=xt[:].rearrange("q c t r -> q c r t"))
             else:
                 nc.scalar.copy(out=grouped[:], in_=xt[:].rearrange("q c t r -> q c r t"))
@@ -422,14 +438,13 @@ def tile_kanlinear_t_kernel(tc, x, coefficients, out):
                     nc.scalar.copy(out=res[:, n * 512 : (n + 1) * 512], in_=acc[:])
             nc.sync.dma_start(out=out_v[t], in_=res[:])
 
-        def pieces(duo, php, chain):
-            at = work.tile([P, 32, W2], BF16, tag="at%s" % chain)
+        def pieces(php, chain):
+            at = work.tile([P, 24, W2], BF16, tag="at%s" % chain)
             f0 = pieces_a(php[0], 0)
             f1 = pieces_a(php[0], 1)
             for q in range(4):
                 pa = pieces_b(f0 if q < 2 else f1, q % 2)
                 pieces_c(at, pa, q)
-            pieces_outer(at, duo)
             return at
 
         ex = ctx.enter_context(tc.tile_pool(name="ex", bufs=1))
@@ -464,9 +479,18 @@ def tile_kanlinear_t_kernel(tc, x, coefficients, out):
             nc.vector.scalar_tensor_tensor(out=tc3[:], in0=qc[:, mirror_rows(1), :], scalar=496.0, in1=tb3[:], op0=ALU.mult, op1=ALU.add)
             nc.vector.scalar_tensor_tensor(out=xec[:, mirror_rows(2), :], in0=qc[:, mirror_rows(0), :], scalar=496.0, in1=ta[:], op0=ALU.mult, op1=ALU.add)
             nc.vector.scalar_tensor_tensor(out=xec[:, mirror_rows(3), :], in0=qc[:, mirror_rows(0), :], scalar=-4960.0, in1=tc3[:], op0=ALU.mult, op1=ALU.add)
+            for first, mm in ((0, mu_pos[4]), (4, mu_neg[4])):
+                nc.vector.tensor_tensor(
+                    out=xec[:, first : first + 4, :],
+                    in0=xec[:, first : first + 4, :],
+                    in1=mm[:, ch * cn : (ch + 1) * cn].unsqueeze(1).to_broadcast([P, 4, cn]),
+                    op=ALU.mult,
+                )
 
-        php_a = powers_scalar(0)
-        php_b = powers_scalar(1)
+        php_a = powers_start(0)
+        php_b = powers_start(1)
+        for k in (4, 3, 2, 1, 0):
+            nc.gpsimd.tensor_scalar(out=mu_neg[k][:], in0=mu_pos[k][:], scalar1=-1.0, scalar2=0.0, op0=ALU.mult, op1=ALU.add)
         taylor_matrix()
         for lv in range(3):
             powers_step(php_a, lv)
@@ -474,12 +498,12 @@ def tile_kanlinear_t_kernel(tc, x, coefficients, out):
         qq_cur = outer_logs(0)
         outer_scalar(qq_cur, 0)
         outer_vector(qq_cur, 0)
-        at_a = pieces(0, php_a, "a")
-        php_a = powers_scalar(2)
+        at_a = pieces(php_a, "a")
+        php_a = powers_start(2)
         for lv in range(3):
             powers_step(php_a, lv)
-        at_b = pieces(1, php_b, "b")
-        php_b = powers_scalar(3)
+        at_b = pieces(php_b, "b")
+        php_b = powers_start(3)
 
         fin_a = None
         fin_b = None
@@ -497,135 +521,132 @@ def tile_kanlinear_t_kernel(tc, x, coefficients, out):
             if m == 0:
                 outer_scalar(qq_cur, 1)
             if finishing:
-                yc0 = turn_a(fin_a, 0)
+                yc0 = turn_a(fin_a, 0, False)
             if preparing:
-                at_a = work.tile([P, 32, W2], BF16, tag="ata")
+                at_a = work.tile([P, 24, W2], BF16, tag="ata")
                 f0 = pieces_a(php_a[0], 0)
             if finishing:
-                yc1 = turn_a(fin_a, 1)
+                yc1 = turn_a(fin_a, 1, False)
                 xt0 = turn_b(yc0)
             if preparing:
                 p0 = pieces_b(f0, 0)
             if finishing:
-                grouped0 = turn_c(xt0, last)
+                grouped0 = turn_c(xt0, last, False)
             if shifting:
-                ga = shift_sign("a", da, 4, old_a)
-                gb = shift_sign("b", db, 4, old_b)
+                ya = first_pick("a", da, old_a)
+                yb = first_pick("b", db, old_b)
             if preparing:
                 powers_step(php_b, 0)
-            if m == 1:
-                quantise_weights()
-            if shifting:
-                ya = shift_pick("a", 4, ga)
-                yb = shift_pick("b", 4, gb)
-            if preparing:
-                powers_step(php_b, 1)
-            if finishing:
-                op0 = quantise(grouped0)
-            if preparing:
                 pieces_c(at_a, p0, 0)
             if finishing:
                 xt1 = turn_b(yc1)
             if preparing:
                 p1 = pieces_b(f0, 1)
             if finishing:
-                yc2 = turn_a(fin_b, 0)
+                yc2 = turn_a(fin_b, 0, last)
             if preparing:
                 f1 = pieces_a(php_a[0], 1)
             if finishing:
-                grouped1 = turn_c(xt1, last)
-                multiply(t0, op0, last)
+                grouped1 = turn_c(xt1, last, False)
             if preparing:
                 pieces_c(at_a, p1, 1)
             if shifting:
                 ga = shift_sign("a", da, 3, ya)
                 gb = shift_sign("b", db, 3, yb)
             if preparing:
-                powers_step(php_b, 2)
-            if finishing:
-                op1 = quantise(grouped1)
+                powers_step(php_b, 1)
             if shifting:
                 ya = shift_pick("a", 3, ga)
                 yb = shift_pick("b", 3, gb)
+            if preparing:
+                powers_step(php_b, 2)
+            if m == 1:
+                quantise_weights()
             if finishing:
                 xt2 = turn_b(yc2)
             if preparing:
                 p2 = pieces_b(f1, 0)
             if finishing:
-                yc3 = turn_a(fin_b, 1)
-                grouped2 = turn_c(xt2, last)
+                yc3 = turn_a(fin_b, 1, last)
+                grouped2 = turn_c(xt2, last, last)
             if preparing:
                 pieces_c(at_a, p2, 2)
             if finishing:
-                multiply(t0 + 1, op1, last)
                 xt3 = turn_b(yc3)
             if preparing:
                 p3 = pieces_b(f1, 1)
             if finishing:
-                grouped3 = turn_c(xt3, last)
+                grouped3 = turn_c(xt3, last, last)
             if preparing:
                 pieces_c(at_a, p3, 3)
-                pieces_outer(at_a, da + 2)
             if ahead:
-                php_a = powers_scalar(da + 4)
+                php_a = powers_start(da + 4)
             if shifting:
                 ga = shift_sign("a", da, 2, ya)
                 gb = shift_sign("b", db, 2, yb)
-            if finishing:
-                op2 = quantise(grouped2)
-            if shifting:
                 ya = shift_pick("a", 2, ga)
                 yb = shift_pick("b", 2, gb)
             if finishing:
-                op3 = quantise(grouped3)
-            if m == 0 or m == 2 or m == 3:
-                outer_vector(qq_cur, 1 if m == 0 else m)
+                op0 = quantise(grouped0)
             if preparing:
-                at_b = work.tile([P, 32, W2], BF16, tag="atb")
+                at_b = work.tile([P, 24, W2], BF16, tag="atb")
                 f0 = pieces_a(php_b[0], 0)
                 f1 = pieces_a(php_b[0], 1)
                 p0 = pieces_b(f0, 0)
             if finishing:
-                multiply(t0 + 2, op2, last)
+                multiply(t0, op0, last)
             if preparing:
                 pieces_c(at_b, p0, 0)
                 p1 = pieces_b(f0, 1)
                 pieces_c(at_b, p1, 1)
+            if shifting:
+                ga = shift_sign("a", da, 1, ya)
+                gb = shift_sign("b", db, 1, yb)
             if finishing:
-                multiply(t0 + 3, op3, last)
+                op1 = quantise(grouped1)
+            if shifting:
+                ya = shift_pick("a", 1, ga)
+                yb = shift_pick("b", 1, gb)
+            if finishing:
+                op2 = quantise(grouped2)
+                multiply(t0 + 1, op1, last)
             if preparing:
                 p2 = pieces_b(f1, 0)
                 pieces_c(at_b, p2, 2)
                 p3 = pieces_b(f1, 1)
                 pieces_c(at_b, p3, 3)
-                pieces_outer(at_b, db + 2)
             if ahead:
-                php_b = powers_scalar(db + 4)
+                php_b = powers_start(db + 4)
+            if finishing:
+                multiply(t0 + 2, op2, last)
+            if shifting:
+                ga = shift_sign("a", da, 0, ya)
+                gb = shift_sign("b", db, 0, yb)
+            if finishing:
+                op3 = quantise(grouped3)
+            if shifting:
+                ya = shift_pick("a", 0, ga)
+                yb = shift_pick("b", 0, gb)
+            if ahead:
+                powers_step(php_a, 0)
+            if finishing:
+                multiply(t0 + 3, op3, last)
             if m == 0:
+                outer_vector(qq_cur, 1)
                 qq_cur = outer_logs(1)
                 for a in range(4, 8):
                     weights_block(a)
             if m == 1 or m == 2:
                 outer_scalar(qq_cur, m + 1)
             if shifting:
-                ga = shift_sign("a", da, 1, ya)
-                gb = shift_sign("b", db, 1, yb)
-            if ahead:
-                powers_step(php_a, 0)
-            if shifting:
-                ya = shift_pick("a", 1, ga)
-                yb = shift_pick("b", 1, gb)
+                ga = flip_sign("a", da, ya)
+                gb = flip_sign("b", db, yb)
             if ahead:
                 powers_step(php_a, 1)
             if shifting:
-                ga = shift_sign("a", da, 0, ya)
-                gb = shift_sign("b", db, 0, yb)
-            if ahead:
-                powers_step(php_a, 2)
-            if shifting:
-                ya = shift_pick("a", 0, ga)
-                yb = shift_pick("b", 0, gb)
-                ga = flip_sign("a", da, ya)
-                gb = flip_sign("b", db, yb)
                 fin_a = flip_pick("a", ga)
                 fin_b = flip_pick("b", gb)
+            if ahead:
+                powers_step(php_a, 2)
+            if m == 2 or m == 3:
+                outer_vector(qq_cur, m)

@@ -144,6 +144,9 @@ def tile_kanlinear_t_kernel(tc, x, coefficients, out):
         w_codes = keep.tile([P, 2, NO], U32, align_bytes=64)
         w_scales = keep.tile([P, 2, NO], U8, align_bytes=64)
         hh = keep.tile([P, NP], F32)
+        h2 = keep.tile([P, NP], F32)
+        h4 = keep.tile([P, NP], F32)
+        h8 = keep.tile([P, NP], F32)
         sg = keep.tile([P, NP], F32)
         sgh = keep.tile([P, NP], F32)
         mu_pos = []
@@ -169,17 +172,12 @@ def tile_kanlinear_t_kernel(tc, x, coefficients, out):
         def weights_block(a):
             cw = wp.tile([P, NI, 32], BF16, tag="cw")
             nc.sync.dma_start(out=cw[:], in_=coef_v[a])
-            cw2 = wp.tile([P, 4, NI, 8], BF16, tag="cw2")
-            if a < 4:
-                nc.scalar.copy(out=cw2[:], in_=cw[:].rearrange("q i (t s) -> q t i s", s=8))
-            else:
-                nc.gpsimd.tensor_scalar(out=cw2[:], in0=cw[:].rearrange("q i (t s) -> q t i s", s=8), scalar1=1.0, scalar2=0.0, op0=ALU.mult, op1=ALU.add)
             wt = psum.tile([P, 2, 4, P], BF16, tag="xt")
             for c in range(2):
                 for tq in range(4):
                     nc.tensor.transpose(
                         out=wt[:, c, tq, :],
-                        in_=cw2[:, tq, c * 16 : (c + 1) * 16, :].rearrange("q i s -> q (i s)"),
+                        in_=cw[:].rearrange("q i d -> q (i d)")[:, c * 512 + tq : (c + 1) * 512 : 4],
                         identity=ident_b[:],
                     )
             nc.scalar.copy(out=gw[:, :, a * P : (a + 1) * P, :], in_=wt[:].rearrange("q c t r -> q c r t"))
@@ -236,6 +234,9 @@ def tile_kanlinear_t_kernel(tc, x, coefficients, out):
                 nc.vector.tensor_scalar(out=s05[:, hs], in0=dj[:, hs], scalar1=0.0, scalar2=0.5, op0=ALU.is_ge, op1=ALU.subtract)
             for hs in halves:
                 nc.vector.scalar_tensor_tensor(out=hh[:, hs], in0=h0[:, hs], scalar=2.0, in1=s05[:, hs], op0=ALU.mult, op1=ALU.mult)
+            nc.scalar.activation(out=h2[:], in_=hh[:], func=ACT.Square)
+            nc.scalar.activation(out=h4[:], in_=h2[:], func=ACT.Square)
+            nc.scalar.activation(out=h8[:], in_=h4[:], func=ACT.Square)
             rr = pre.tile([P, NP], F32, tag="rot", bufs=3)
             for hs in halves:
                 nc.vector.scalar_tensor_tensor(out=rr[:, hs], in0=dj[:, hs], scalar=2.0, in1=s05[:, hs], op0=ALU.mult, op1=ALU.mult)
@@ -251,10 +252,12 @@ def tile_kanlinear_t_kernel(tc, x, coefficients, out):
                     nc.vector.tensor_scalar(out=sg[:], in0=bit_prev[:], scalar1=-2.0, scalar2=1.0, op0=ALU.mult, op1=ALU.add)
                 if k < 4:
                     nc.vector.tensor_scalar(out=mu_pos[k + 1][:], in0=bit_prev[:], scalar1=-2.0, scalar2=1.0, op0=ALU.mult, op1=ALU.add)
+                    nc.vector.tensor_scalar(out=mu_neg[k + 1][:], in0=bit_prev[:], scalar1=2.0, scalar2=-1.0, op0=ALU.mult, op1=ALU.add)
                 if k == 2:
                     nc.vector.tensor_tensor(out=sgh[:], in0=sg[:], in1=hh[:], op=ALU.mult)
                 bit_prev = bit
             nc.vector.tensor_scalar(out=mu_pos[0][:], in0=bit_prev[:], scalar1=-2.0, scalar2=1.0, op0=ALU.mult, op1=ALU.add)
+            nc.vector.tensor_scalar(out=mu_neg[0][:], in0=bit_prev[:], scalar1=2.0, scalar2=-1.0, op0=ALU.mult, op1=ALU.add)
 
         work = ctx.enter_context(tc.tile_pool(name="work", bufs=2))
 
@@ -305,22 +308,17 @@ def tile_kanlinear_t_kernel(tc, x, coefficients, out):
 
         def powers_start(duo):
             ph = work.tile([P, NG, NPW, NG], F32, tag="ph")
-            pw = work.tile([P, NG, 3, NG], F32, tag="pw")
-            hv = pair_view(hh, duo * W2)
-            nc.gpsimd.tensor_copy(out=ph[:, :, 0, :], in_=pair_view(sg, duo * W2))
-            nc.gpsimd.tensor_tensor(out=pw[:, :, 0, :], in0=hv, in1=hv, op=ALU.mult)
-            nc.gpsimd.tensor_copy(out=ph[:, :, 1, :], in_=pair_view(sgh, duo * W2))
-            for lv in range(1, 3):
-                nc.gpsimd.tensor_tensor(out=pw[:, :, lv, :], in0=pw[:, :, lv - 1, :], in1=pw[:, :, lv - 1, :], op=ALU.mult)
-            return (ph, pw)
+            nc.scalar.copy(out=ph[:, :, 0, :], in_=pair_view(sg, duo * W2))
+            nc.scalar.copy(out=ph[:, :, 1, :], in_=pair_view(sgh, duo * W2))
+            return (ph, duo)
 
         def powers_step(php, lv):
-            ph, pw = php
+            ph, duo = php
             n = 2 << lv
             nc.vector.tensor_tensor(
                 out=ph[:, :, n : 2 * n, :],
                 in0=ph[:, :, 0:n, :],
-                in1=pw[:, :, lv, :].unsqueeze(2).to_broadcast([P, NG, n, NG]),
+                in1=pair_view((h2, h4, h8)[lv], duo * W2).unsqueeze(2).to_broadcast([P, NG, n, NG]),
                 op=ALU.mult,
             )
 
@@ -389,9 +387,9 @@ def tile_kanlinear_t_kernel(tc, x, coefficients, out):
         def turn_a(yfin, a, swap):
             yc = work.tile([P, 4, NI, 8], BF16, tag="yc")
             if swap:
-                nc.vector.tensor_copy(out=yc[:], in_=yfin[:, 0:32, a * NI : (a + 1) * NI].rearrange("q (t s) i -> q t i s", s=8))
+                nc.vector.tensor_copy(out=yc[:], in_=yfin[:, 0:32, a * NI : (a + 1) * NI].rearrange("q (s t) i -> q t i s", t=4))
             else:
-                nc.scalar.activation(out=yc[:], in_=yfin[:, 0:32, a * NI : (a + 1) * NI].rearrange("q (t s) i -> q t i s", s=8), func=ACT.Abs)
+                nc.scalar.activation(out=yc[:], in_=yfin[:, 0:32, a * NI : (a + 1) * NI].rearrange("q (s t) i -> q t i s", t=4), func=ACT.Abs)
             return yc
 
         def turn_b(yc):
@@ -489,8 +487,6 @@ def tile_kanlinear_t_kernel(tc, x, coefficients, out):
 
         php_a = powers_start(0)
         php_b = powers_start(1)
-        for k in (4, 3, 2, 1, 0):
-            nc.gpsimd.tensor_scalar(out=mu_neg[k][:], in0=mu_pos[k][:], scalar1=-1.0, scalar2=0.0, op0=ALU.mult, op1=ALU.add)
         taylor_matrix()
         for lv in range(3):
             powers_step(php_a, lv)
@@ -560,8 +556,6 @@ def tile_kanlinear_t_kernel(tc, x, coefficients, out):
                 yb = shift_pick("b", 3, gb)
             if preparing:
                 powers_step(php_b, 2)
-            if m == 1:
-                quantise_weights()
             if finishing:
                 xt2 = turn_b(yc2)
             if preparing:
@@ -586,6 +580,8 @@ def tile_kanlinear_t_kernel(tc, x, coefficients, out):
                 gb = shift_sign("b", db, 2, yb)
                 ya = shift_pick("a", 2, ga)
                 yb = shift_pick("b", 2, gb)
+            if m == 1:
+                quantise_weights()
             if finishing:
                 op0 = quantise(grouped0)
             if preparing:

@@ -384,12 +384,16 @@ def tile_kanlinear_t_kernel(tc, x, coefficients, out):
             nc.vector.tensor_tensor(out=yfin[:, 1:32:2, :], in0=gcur[:, 1:32:2, :], in1=gcur[:, 30::-2, :], op=ALU.min)
             return yfin
 
-        def turn_a(yfin, a, swap):
-            yc = work.tile([P, 4, NI, 8], BF16, tag="yc")
-            if swap:
-                nc.vector.tensor_copy(out=yc[:], in_=yfin[:, 0:32, a * NI : (a + 1) * NI].rearrange("q (s t) i -> q t i s", t=4))
-            else:
-                nc.scalar.activation(out=yc[:], in_=yfin[:, 0:32, a * NI : (a + 1) * NI].rearrange("q (s t) i -> q t i s", t=4), func=ACT.Abs)
+        def turn_a(yfin, a):
+            yc = work.tile([P, 4, NI, 8], BF16, tag="yc", bufs=4)
+            nc.scalar.activation(out=yc[:], in_=yfin[:, 0:32, a * NI : (a + 1) * NI].rearrange("q (s t) i -> q t i s", t=4), func=ACT.Abs)
+            return yc
+
+        def turn_a_vector(yfin, a):
+            yc = work.tile([P, 4, NI, 8], BF16, tag="yc", bufs=4)
+            rows = yfin[:, 0:32, a * NI : (a + 1) * NI].rearrange("q (s t) i -> q t i s", t=4)
+            nc.vector.tensor_copy(out=yc[:, 0:4:2, :, :], in_=rows[:, 0:4:2, :, :])
+            nc.vector.tensor_scalar_mul(out=yc[:, 1:4:2, :, :], in0=rows[:, 1:4:2, :, :], scalar1=-1.0)
             return yc
 
         def turn_b(yc):
@@ -399,14 +403,14 @@ def tile_kanlinear_t_kernel(tc, x, coefficients, out):
                     nc.tensor.transpose(out=xt[:, c, tq, :], in_=yc[:, tq, c * 16 : (c + 1) * 16, :].rearrange("q i s -> q (i s)"), identity=ident_b[:])
             return xt
 
-        def turn_c(xt, last, swap):
+        def turn_c(xt):
             grouped = work.tile([P, 2, P, 4], BF16, tag="grouped", align_bytes=64, bufs=4)
-            if swap:
-                nc.scalar.activation(out=grouped[:], in_=xt[:].rearrange("q c t r -> q c r t"), func=ACT.Abs)
-            elif last:
-                nc.vector.tensor_copy(out=grouped[:], in_=xt[:].rearrange("q c t r -> q c r t"))
-            else:
-                nc.scalar.copy(out=grouped[:], in_=xt[:].rearrange("q c t r -> q c r t"))
+            nc.scalar.copy(out=grouped[:], in_=xt[:].rearrange("q c t r -> q c r t"))
+            return grouped
+
+        def turn_c_vector(xt):
+            grouped = work.tile([P, 2, P, 4], BF16, tag="grouped", align_bytes=64, bufs=4)
+            nc.vector.tensor_copy(out=grouped[:], in_=xt[:].rearrange("q c t r -> q c r t"))
             return grouped
 
         def quantise(grouped):
@@ -415,9 +419,9 @@ def tile_kanlinear_t_kernel(tc, x, coefficients, out):
             nc.vector.quantize_mx(out=b_codes[:].bitcast(FP8X4), scales=b_scales[:], in_=grouped[:].rearrange("q c r t -> q (c r t)"))
             return (b_codes, b_scales)
 
-        def multiply(t, operand, last):
+        def multiply(t, operand, shared):
             b_codes, b_scales = operand
-            res = work.tile([P, NO], F32, tag="res")
+            res = work.tile([P, NO], F32, tag="res", bufs=4)
             for n in range(2):
                 acc = psum.tile([P, 512], F32, tag="acc")
                 for c in range(2):
@@ -430,7 +434,7 @@ def tile_kanlinear_t_kernel(tc, x, coefficients, out):
                         start=(c == 0),
                         stop=(c == 1),
                     )
-                if last and n == 1:
+                if shared and n == 1:
                     nc.vector.tensor_copy(out=res[:, n * 512 : (n + 1) * 512], in_=acc[:])
                 else:
                     nc.scalar.copy(out=res[:, n * 512 : (n + 1) * 512], in_=acc[:])
@@ -503,12 +507,11 @@ def tile_kanlinear_t_kernel(tc, x, coefficients, out):
 
         fin_a = None
         fin_b = None
-        for m in range(NQ + 1):
-            shifting = m < NQ
+        for m in range(NQ):
+            shifting = True
             finishing = m >= 1
             preparing = m + 1 < NQ
             ahead = m + 2 < NQ
-            last = m == NQ
             da = 2 * m
             db = 2 * m + 1
             t0 = 4 * (m - 1)
@@ -517,17 +520,17 @@ def tile_kanlinear_t_kernel(tc, x, coefficients, out):
             if m == 0:
                 outer_scalar(qq_cur, 1)
             if finishing:
-                yc0 = turn_a(fin_a, 0, False)
+                yc0 = turn_a(fin_a, 0)
             if preparing:
                 at_a = work.tile([P, 24, W2], BF16, tag="ata")
                 f0 = pieces_a(php_a[0], 0)
             if finishing:
-                yc1 = turn_a(fin_a, 1, False)
+                yc1 = turn_a(fin_a, 1)
                 xt0 = turn_b(yc0)
             if preparing:
                 p0 = pieces_b(f0, 0)
             if finishing:
-                grouped0 = turn_c(xt0, last, False)
+                grouped0 = turn_c(xt0)
             if shifting:
                 ya = first_pick("a", da, old_a)
                 yb = first_pick("b", db, old_b)
@@ -539,11 +542,11 @@ def tile_kanlinear_t_kernel(tc, x, coefficients, out):
             if preparing:
                 p1 = pieces_b(f0, 1)
             if finishing:
-                yc2 = turn_a(fin_b, 0, last)
+                yc2 = turn_a(fin_b, 0)
             if preparing:
                 f1 = pieces_a(php_a[0], 1)
             if finishing:
-                grouped1 = turn_c(xt1, last, False)
+                grouped1 = turn_c(xt1)
             if preparing:
                 pieces_c(at_a, p1, 1)
             if shifting:
@@ -561,8 +564,8 @@ def tile_kanlinear_t_kernel(tc, x, coefficients, out):
             if preparing:
                 p2 = pieces_b(f1, 0)
             if finishing:
-                yc3 = turn_a(fin_b, 1, last)
-                grouped2 = turn_c(xt2, last, last)
+                yc3 = turn_a(fin_b, 1)
+                grouped2 = turn_c(xt2)
             if preparing:
                 pieces_c(at_a, p2, 2)
             if finishing:
@@ -570,7 +573,7 @@ def tile_kanlinear_t_kernel(tc, x, coefficients, out):
             if preparing:
                 p3 = pieces_b(f1, 1)
             if finishing:
-                grouped3 = turn_c(xt3, last, last)
+                grouped3 = turn_c(xt3)
             if preparing:
                 pieces_c(at_a, p3, 3)
             if ahead:
@@ -590,7 +593,7 @@ def tile_kanlinear_t_kernel(tc, x, coefficients, out):
                 f1 = pieces_a(php_b[0], 1)
                 p0 = pieces_b(f0, 0)
             if finishing:
-                multiply(t0, op0, last)
+                multiply(t0, op0, False)
             if preparing:
                 pieces_c(at_b, p0, 0)
                 p1 = pieces_b(f0, 1)
@@ -605,7 +608,7 @@ def tile_kanlinear_t_kernel(tc, x, coefficients, out):
                 yb = shift_pick("b", 1, gb)
             if finishing:
                 op2 = quantise(grouped2)
-                multiply(t0 + 1, op1, last)
+                multiply(t0 + 1, op1, False)
             if preparing:
                 p2 = pieces_b(f1, 0)
                 pieces_c(at_b, p2, 2)
@@ -614,7 +617,7 @@ def tile_kanlinear_t_kernel(tc, x, coefficients, out):
             if ahead:
                 php_b = powers_start(db + 4)
             if finishing:
-                multiply(t0 + 2, op2, last)
+                multiply(t0 + 2, op2, False)
             if shifting:
                 ga = shift_sign("a", da, 0, ya)
                 gb = shift_sign("b", db, 0, yb)
@@ -626,7 +629,7 @@ def tile_kanlinear_t_kernel(tc, x, coefficients, out):
             if ahead:
                 powers_step(php_a, 0)
             if finishing:
-                multiply(t0 + 3, op3, last)
+                multiply(t0 + 3, op3, False)
             if m == 0:
                 outer_vector(qq_cur, 1)
                 qq_cur = outer_logs(1)
@@ -646,3 +649,21 @@ def tile_kanlinear_t_kernel(tc, x, coefficients, out):
                 powers_step(php_a, 2)
             if m == 2 or m == 3:
                 outer_vector(qq_cur, m)
+
+        t0 = NT - 4
+        yc0 = turn_a(fin_a, 0)
+        yc2 = turn_a_vector(fin_b, 0)
+        yc1 = turn_a(fin_a, 1)
+        yc3 = turn_a_vector(fin_b, 1)
+        xt2 = turn_b(yc2)
+        xt0 = turn_b(yc0)
+        op2 = quantise(turn_c_vector(xt2))
+        xt3 = turn_b(yc3)
+        multiply(t0 + 2, op2, False)
+        op0 = quantise(turn_c_vector(xt0))
+        xt1 = turn_b(yc1)
+        op3 = quantise(turn_c_vector(xt3))
+        multiply(t0, op0, False)
+        op1 = quantise(turn_c_vector(xt1))
+        multiply(t0 + 3, op3, True)
+        multiply(t0 + 1, op1, True)

from contextlib import ExitStack

import concourse.mybir as mybir
from concourse.masks import make_identity

FLOPS = 2 * 4096 * 1024 * 1024

F32 = mybir.dt.float32
BF16 = mybir.dt.bfloat16
I32 = mybir.dt.int32
U32 = mybir.dt.uint32
U8 = mybir.dt.uint8
FP8X4 = mybir.dt.float8_e4m3fn_x4
ACT = mybir.ActivationFunctionType
ALU = mybir.AluOpType
AX = mybir.AxisListType

P = 128
NB = 4096
NI = 32
NO = 1024
NT = NB // P
NP = NT * NI
ND = NT // 2
NQ = ND // 2
W2 = 2 * NI
ROWS = 64
UMAX = 62.99999
NPW = 16
NG = P // NPW
NLO = 8


def binomial(n, k):
    v = 1
    for j in range(k):
        v = v * (n - j) // (j + 1)
    return v


def factorial31():
    v = 1
    for j in range(2, 32):
        v = v * j
    return v


def taylor_coefficient(r, p):
    total = 0
    for k in range(r + 1):
        total += (-1) ** k * binomial(32, k) * (2 * (r - k) + 1) ** (31 - p)
    return float(binomial(31, p) * total) / float(factorial31() * 2 ** (31 - p))


def to_float32(v):
    if v == 0.0:
        return 0.0
    s = abs(v)
    e = 0
    while s >= 2.0:
        s = s / 2.0
        e += 1
    while s < 1.0:
        s = s * 2.0
        e -= 1
    m = float(round(s * 8388608.0)) * 2.0 ** (e - 23)
    return m if v > 0.0 else -m


def mirror_rows(m):
    return slice(m, 8 - m, 7 - 2 * m)


def chi(k, e):
    return 1 if ((e >> k) & 1) == 0 else -1


def row_groups(lo, hi, sign_of, want):
    runs = []
    e = lo
    while e < hi:
        if sign_of(e) == want:
            s = e
            while e < hi and sign_of(e) == want:
                e += 1
            runs.append((s, e - s))
        else:
            e += 1
    groups = []
    for ln in sorted(set([r[1] for r in runs])):
        starts = [r[0] for r in runs if r[1] == ln]
        n = 0
        while n < len(starts):
            cnt = 1
            per = 0
            while n + cnt < len(starts):
                step = starts[n + cnt] - starts[n + cnt - 1]
                if cnt == 1:
                    per = step
                if step != per:
                    break
                cnt += 1
            if cnt == 1:
                per = 0
            groups.append((starts[n], ln, cnt, per))
            n += cnt
    return groups


def rows_view(buf, grp, shift):
    s, ln, cnt, per = grp
    s = s - shift
    if cnt == 1:
        return buf[:, s : s + ln, :]
    return buf[:, s : s + cnt * per, :].rearrange("q (z r) w -> q z r w", r=per)[:, :, 0:ln, :]


def pair_rows(arr, p0, grp):
    s, ln, cnt, per = grp
    v = arr[:, p0 : p0 + W2].unsqueeze(1)
    if cnt == 1:
        return v.to_broadcast([P, ln, W2])
    return v.unsqueeze(1).to_broadcast([P, cnt, ln, W2])


def tile_kanlinear_t_kernel(tc, x, coefficients, out):
    nc = tc.nc
    c31 = pow(float(factorial31()), -1.0 / 31.0)
    out_v = out.rearrange("(p t) o -> t p o", t=NT)
    coef_v = coefficients.rearrange("i (a o) d -> a o i d", o=P)

    with ExitStack() as ctx:
        ctx.enter_context(tc.manual_schedule())
        keep = ctx.enter_context(tc.tile_pool(name="keep", bufs=1))
        psum = ctx.enter_context(tc.psum_pool(name="psum", bufs=2))
        wp = ctx.enter_context(tc.tile_pool(name="wp", bufs=2))

        ident_f = keep.tile([P, P], F32)
        make_identity(nc, ident_f[:])
        ident_b = keep.tile([P, P], BF16)
        make_identity(nc, ident_b[:])

        wmat = keep.tile([P, 24, NG], F32)
        w_codes = keep.tile([P, 2, NO], U32, align_bytes=64)
        w_scales = keep.tile([P, 2, NO], U8, align_bytes=64)
        hh = keep.tile([P, NP], F32)
        h2 = keep.tile([P, NP], F32)
        h4 = keep.tile([P, NP], F32)
        h8 = keep.tile([P, NP], F32)
        sg = keep.tile([P, NP], F32)
        sgh = keep.tile([P, NP], F32)
        mu_pos = []
        mu_neg = []
        for k in range(5):
            mu_pos.append(keep.tile([P, NP], BF16, name="mu_pos%d" % k))
            mu_neg.append(keep.tile([P, NP], BF16, name="mu_neg%d" % k))
        mn_pos = keep.tile([P, NP], BF16)
        xe = keep.tile([P, 8, NP], BF16)

        tb_hi = keep.tile([P, 12, NPW], F32)
        tb_lo = keep.tile([P, 12, NLO], F32)
        for p in range(NPW):
            for r in range(4, 16):
                v = taylor_coefficient(r, p)
                hi = to_float32(v)
                nc.gpsimd.memset(tb_hi[:, r - 4, p : p + 1], hi)
                if p < NLO:
                    nc.vector.memset(tb_lo[:, r - 4, p : p + 1], to_float32(v - hi))

        gw = wp.tile([P, 2, NO, 4], BF16, align_bytes=64, bufs=1)

        def weights_block(a):
            cw = wp.tile([P, NI, 32], BF16, tag="cw")
            nc.sync.dma_start(out=cw[:], in_=coef_v[a])
            wt = psum.tile([P, 2, 4, P], BF16, tag="xt")
            for c in range(2):
                for tq in range(4):
                    nc.tensor.transpose(
                        out=wt[:, c, tq, :],
                        in_=cw[:].rearrange("q i d -> q (i d)")[:, c * 512 + tq : (c + 1) * 512 : 4],
                        identity=ident_b[:],
                    )
            nc.scalar.copy(out=gw[:, :, a * P : (a + 1) * P, :], in_=wt[:].rearrange("q c t r -> q c r t"))

        with tc.tile_pool(name="pre", bufs=1) as pre:
            halves = (slice(0, NP // 2), slice(NP // 2, NP))
            xb = pre.tile([P, NP], BF16)
            nc.sync.dma_start(out=xb[:], in_=x.rearrange("(p t) i -> p (t i)", t=NT))
            th = pre.tile([P, NP], F32, tag="rot", bufs=3)
            for hs in halves:
                nc.scalar.activation(out=th[:, hs], in_=xb[:, hs], func=ACT.Tanh)

            for a in range(4):
                weights_block(a)

            u0 = pre.tile([P, NP], F32, tag="rot", bufs=3)
            for hs in halves:
                nc.vector.tensor_scalar(out=u0[:, hs], in0=th[:, hs], scalar1=31.5, scalar2=31.5, op0=ALU.mult, op1=ALU.add)
            uu = pre.tile([P, NP], F32)
            for hs in halves:
                nc.vector.tensor_scalar(out=uu[:, hs], in0=u0[:, hs], scalar1=UMAX, scalar2=0.0, op0=ALU.min, op1=ALU.max)
            ji = pre.tile([P, NP], I32)
            for hs in halves:
                nc.vector.tensor_copy(out=ji[:, hs], in_=uu[:, hs])
            jf = pre.tile([P, NP], F32, tag="rot", bufs=3)
            for hs in halves:
                nc.vector.tensor_copy(out=jf[:, hs], in_=ji[:, hs])
            fr = pre.tile([P, NP], F32, tag="rot", bufs=3)
            for hs in halves:
                nc.vector.tensor_tensor(out=fr[:, hs], in0=uu[:, hs], in1=jf[:, hs], op=ALU.subtract)
            j1a = pre.tile([P, NP], F32, tag="rot", bufs=3)
            for hs in halves:
                nc.vector.scalar_tensor_tensor(out=j1a[:, hs], in0=fr[:, hs], scalar=1.0, in1=jf[:, hs], op0=ALU.is_ge, op1=ALU.add)
            j1b = pre.tile([P, NP], F32, tag="rot", bufs=3)
            for hs in halves:
                nc.vector.scalar_tensor_tensor(out=j1b[:, hs], in0=fr[:, hs], scalar=0.0, in1=j1a[:, hs], op0=ALU.is_ge, op1=ALU.add)
            j1i = pre.tile([P, NP], I32)
            for hs in halves:
                nc.vector.tensor_copy(out=j1i[:, hs], in_=j1b[:, hs])
            j1 = pre.tile([P, NP], F32, tag="rot", bufs=3)
            for hs in halves:
                nc.vector.tensor_copy(out=j1[:, hs], in_=j1i[:, hs])
            hm = pre.tile([P, NP], F32, tag="rot", bufs=3)
            for hs in halves:
                nc.vector.tensor_tensor(out=hm[:, hs], in0=uu[:, hs], in1=j1[:, hs], op=ALU.subtract)
            h0 = pre.tile([P, NP], F32, tag="rot", bufs=3)
            for hs in halves:
                nc.vector.tensor_scalar_add(out=h0[:, hs], in0=hm[:, hs], scalar1=0.5)
            dj = pre.tile([P, NP], F32)
            for hs in halves:
                nc.vector.tensor_scalar_add(out=dj[:, hs], in0=j1[:, hs], scalar1=-32.0)
            s05 = pre.tile([P, NP], F32)
            for hs in halves:
                nc.vector.tensor_scalar(out=s05[:, hs], in0=dj[:, hs], scalar1=0.0, scalar2=0.5, op0=ALU.is_ge, op1=ALU.subtract)
            for hs in halves:
                nc.vector.scalar_tensor_tensor(out=hh[:, hs], in0=h0[:, hs], scalar=2.0, in1=s05[:, hs], op0=ALU.mult, op1=ALU.mult)
            nc.scalar.activation(out=h2[:], in_=hh[:], func=ACT.Square)
            nc.scalar.activation(out=h4[:], in_=h2[:], func=ACT.Square)
            nc.scalar.activation(out=h8[:], in_=h4[:], func=ACT.Square)
            rr = pre.tile([P, NP], F32, tag="rot", bufs=3)
            for hs in halves:
                nc.vector.scalar_tensor_tensor(out=rr[:, hs], in0=dj[:, hs], scalar=2.0, in1=s05[:, hs], op0=ALU.mult, op1=ALU.mult)
            ri = pre.tile([P, NP], I32)
            for hs in halves:
                nc.vector.tensor_copy(out=ri[:, hs], in_=rr[:, hs])
            nc.vector.tensor_scalar_mul(out=mn_pos[:], in0=s05[:], scalar1=2.0)
            bit_prev = None
            for k in (4, 3, 2, 1, 0):
                bit = pre.tile([P, NP], I32, tag="bit", bufs=3)
                nc.vector.tensor_scalar(out=bit[:], in0=ri[:], scalar1=k, scalar2=1, op0=ALU.logical_shift_right, op1=ALU.bitwise_and)
                if k == 3:
                    nc.vector.tensor_scalar(out=sg[:], in0=bit_prev[:], scalar1=-2.0, scalar2=1.0, op0=ALU.mult, op1=ALU.add)
                if k < 4:
                    nc.vector.tensor_scalar(out=mu_pos[k + 1][:], in0=bit_prev[:], scalar1=-2.0, scalar2=1.0, op0=ALU.mult, op1=ALU.add)
                    nc.vector.tensor_scalar(out=mu_neg[k + 1][:], in0=bit_prev[:], scalar1=2.0, scalar2=-1.0, op0=ALU.mult, op1=ALU.add)
                if k == 2:
                    nc.vector.tensor_tensor(out=sgh[:], in0=sg[:], in1=hh[:], op=ALU.mult)
                bit_prev = bit
            nc.vector.tensor_scalar(out=mu_pos[0][:], in0=bit_prev[:], scalar1=-2.0, scalar2=1.0, op0=ALU.mult, op1=ALU.add)
            nc.vector.tensor_scalar(out=mu_neg[0][:], in0=bit_prev[:], scalar1=2.0, scalar2=-1.0, op0=ALU.mult, op1=ALU.add)

        work = ctx.enter_context(tc.tile_pool(name="work", bufs=2))

        def pair_view(arr, p0):
            return arr[:, p0 : p0 + W2].rearrange("q (c g) -> q c g", g=NG)

        def taylor_matrix():
            lo_part = tb_hi[:, :, 0:NLO]
            nc.vector.tensor_tensor(out=lo_part, in0=lo_part, in1=tb_lo[:], op=ALU.add)
            dmask = wp.tile([P, NPW], F32, bufs=1)
            nc.vector.tensor_reduce(out=dmask[:], in_=ident_f[:].rearrange("q (p g) -> q p g", g=NG), axis=AX.X, op=ALU.add)
            gmask = wp.tile([P, NG], F32, bufs=1)
            nc.vector.tensor_reduce(out=gmask[:], in_=ident_f[:].rearrange("q (p g) -> q g p", g=NG), axis=AX.X, op=ALU.add)
            alt = wp.tile([P, NPW], F32, bufs=1)
            nc.vector.memset(alt[:], 1.0)
            nc.vector.memset(alt[:, 1:NPW:2], -1.0)
            sa = wp.tile([P, NPW], F32, bufs=1)
            nc.vector.tensor_tensor(out=sa[:], in0=dmask[:], in1=alt[:], op=ALU.mult)
            sgnp = wp.tile([P, 1], F32, bufs=1)
            nc.vector.tensor_reduce(out=sgnp[:], in_=sa[:], axis=AX.X, op=ALU.add)
            t1 = wp.tile([P, 12, NPW], F32, bufs=1)
            nc.vector.tensor_tensor(
                out=t1[:],
                in0=tb_hi[:],
                in1=dmask[:].unsqueeze(1).to_broadcast([P, 12, NPW]),
                op=ALU.mult,
            )
            w0 = wp.tile([P, 12], F32, bufs=1)
            nc.vector.tensor_reduce(out=w0[:], in_=t1[:], axis=AX.X, op=ALU.add)
            wc = wp.tile([P, 24], F32, bufs=1)
            nc.vector.tensor_scalar(out=wc[:, 0:12], in0=w0[:], scalar1=sgnp[:, 0:1], scalar2=None, op0=ALU.mult)
            for e in range(16, 28):
                nc.vector.tensor_scalar_mul(out=wc[:, e - 4 : e - 3], in0=w0[:, 27 - e : 28 - e], scalar1=-1.0)
            nc.vector.tensor_tensor(
                out=wmat[:],
                in0=wc[:].unsqueeze(2).to_broadcast([P, 24, NG]),
                in1=gmask[:].unsqueeze(1).to_broadcast([P, 24, NG]),
                op=ALU.mult,
            )

        def quantise_weights():
            for c in range(2):
                nc.vector.quantize_mx(
                    out=w_codes[:, c, :].bitcast(FP8X4),
                    scales=w_scales[:, c, :],
                    in_=gw[:, c, :, :].rearrange("q o t -> q (o t)"),
                )

        def powers_start(duo):
            ph = work.tile([P, NG, NPW, NG], F32, tag="ph")
            nc.scalar.copy(out=ph[:, :, 0, :], in_=pair_view(sg, duo * W2))
            nc.scalar.copy(out=ph[:, :, 1, :], in_=pair_view(sgh, duo * W2))
            return (ph, duo)

        def powers_step(php, lv):
            ph, duo = php
            n = 2 << lv
            nc.vector.tensor_tensor(
                out=ph[:, :, n : 2 * n, :],
                in0=ph[:, :, 0:n, :],
                in1=pair_view((h2, h4, h8)[lv], duo * W2).unsqueeze(2).to_broadcast([P, NG, n, NG]),
                op=ALU.mult,
            )

        def pieces_a(ph, hq):
            ft = psum.tile([P, 4, P], F32, tag="ft")
            for s in range(4):
                nc.tensor.transpose(out=ft[:, s, :], in_=ph[:, hq * 4 + s, :, :].rearrange("q p g -> q (p g)"), identity=ident_f[:])
            fts = work.tile([P, 4, P], F32, tag="fts")
            nc.scalar.copy(out=fts[:], in_=ft[:])
            return fts

        def pieces_b(fts, j):
            pa = psum.tile([P, 512], F32, tag="pa")
            for s in range(2):
                nc.tensor.matmul(out=pa[:, s * 192 : (s + 1) * 192], lhsT=fts[:, 2 * j + s, :], rhs=wmat[:].rearrange("q e g -> q (e g)"), start=True, stop=True)
            return pa

        def pieces_c(at, pa, q):
            nc.scalar.copy(
                out=at[:, :, q * 16 : (q + 1) * 16].rearrange("q e (s g) -> q e s g", g=NG),
                in_=pa[:, 0:384].rearrange("q (s e g) -> q e s g", s=2, e=24, g=NG),
            )

        def signed(chain, duo, src, pattern, m_pos, m_neg):
            gcur = work.tile([P, ROWS, W2], BF16, tag="gs%s" % chain, bufs=1)
            for want, mm in ((1, m_pos), (-1, m_neg)):
                for grp in row_groups(0, 32, pattern, want):
                    nc.vector.tensor_tensor(out=rows_view(gcur, grp, 0), in0=rows_view(src, grp, 0), in1=pair_rows(mm, duo * W2, grp), op=ALU.mult)
            return gcur

        def shift_sign(chain, duo, k, src):
            return signed(chain, duo, src, lambda e: chi(k + 1, e) * chi(k, e), mu_pos[k], mu_neg[k])

        def shift_pick(chain, k, gcur):
            a = 1 << k
            ycur = work.tile([P, ROWS, W2], BF16, tag="ys%s" % chain, bufs=1)
            nc.vector.tensor_scalar_max(out=ycur[:, 0:a, :], in0=gcur[:, 0:a, :], scalar1=0.0)
            for want, op in ((1, ALU.max), (-1, ALU.min)):
                for grp in row_groups(a, 32, lambda e: chi(k, e), want):
                    nc.vector.tensor_tensor(out=rows_view(ycur, grp, 0), in0=rows_view(gcur, grp, 0), in1=rows_view(gcur, grp, a), op=op)
            return ycur

        def first_pick(chain, duo, at):
            lo = xe[:, 0:4, duo * W2 : (duo + 1) * W2]
            hi = xe[:, 4:8, duo * W2 : (duo + 1) * W2]
            ycur = work.tile([P, ROWS, W2], BF16, tag="ys%s" % chain, bufs=1)
            nc.vector.tensor_scalar_max(out=ycur[:, 0:4, :], in0=lo, scalar1=0.0)
            nc.vector.tensor_scalar_max(out=ycur[:, 4:16, :], in0=at[:, 0:12, :], scalar1=0.0)
            nc.vector.tensor_tensor(out=ycur[:, 16:20, :], in0=at[:, 12:16, :], in1=lo, op=ALU.min)
            nc.vector.tensor_tensor(out=ycur[:, 20:28, :], in0=at[:, 16:24, :], in1=at[:, 0:8, :], op=ALU.min)
            nc.vector.tensor_tensor(out=ycur[:, 28:32, :], in0=hi, in1=at[:, 8:12, :], op=ALU.min)
            return ycur

        def flip_sign(chain, duo, src):
            gcur = work.tile([P, ROWS, W2], BF16, tag="gs%s" % chain, bufs=1)
            grp = (0, 32, 1, 0)
            nc.vector.tensor_tensor(out=rows_view(gcur, grp, 0), in0=rows_view(src, grp, 0), in1=pair_rows(mn_pos, duo * W2, grp), op=ALU.mult)
            return gcur

        def flip_pick(chain, gcur):
            yfin = work.tile([P, 32, W2], BF16, tag="yfin%s" % chain)
            nc.vector.tensor_tensor(out=yfin[:, 0:32:2, :], in0=gcur[:, 0:32:2, :], in1=gcur[:, 31::-2, :], op=ALU.max)
            nc.vector.tensor_tensor(out=yfin[:, 1:32:2, :], in0=gcur[:, 1:32:2, :], in1=gcur[:, 30::-2, :], op=ALU.min)
            return yfin

        def turn_a(yfin, a):
            yc = work.tile([P, 4, NI, 8], BF16, tag="yc", bufs=4)
            nc.scalar.activation(out=yc[:], in_=yfin[:, 0:32, a * NI : (a + 1) * NI].rearrange("q (s t) i -> q t i s", t=4), func=ACT.Abs)
            return yc

        def turn_a_vector(yfin, a):
            yc = work.tile([P, 4, NI, 8], BF16, tag="yc", bufs=4)
            rows = yfin[:, 0:32, a * NI : (a + 1) * NI].rearrange("q (s t) i -> q t i s", t=4)
            nc.vector.tensor_copy(out=yc[:, 0:4:2, :, :], in_=rows[:, 0:4:2, :, :])
            nc.vector.tensor_scalar_mul(out=yc[:, 1:4:2, :, :], in0=rows[:, 1:4:2, :, :], scalar1=-1.0)
            return yc

        def turn_b(yc):
            xt = psum.tile([P, 2, 4, P], BF16, tag="xt")
            for c in range(2):
                for tq in range(4):
                    nc.tensor.transpose(out=xt[:, c, tq, :], in_=yc[:, tq, c * 16 : (c + 1) * 16, :].rearrange("q i s -> q (i s)"), identity=ident_b[:])
            return xt

        def turn_c(xt):
            grouped = work.tile([P, 2, P, 4], BF16, tag="grouped", align_bytes=64, bufs=4)
            nc.scalar.copy(out=grouped[:], in_=xt[:].rearrange("q c t r -> q c r t"))
            return grouped

        def turn_c_vector(xt):
            grouped = work.tile([P, 2, P, 4], BF16, tag="grouped", align_bytes=64, bufs=4)
            nc.vector.tensor_copy(out=grouped[:], in_=xt[:].rearrange("q c t r -> q c r t"))
            return grouped

        def quantise(grouped):
            b_codes = work.tile([P, 2 * P], U32, tag="b_codes", align_bytes=64, bufs=4)
            b_scales = work.tile([P, 2 * P], U8, tag="b_scales", align_bytes=64, bufs=4)
            nc.vector.quantize_mx(out=b_codes[:].bitcast(FP8X4), scales=b_scales[:], in_=grouped[:].rearrange("q c r t -> q (c r t)"))
            return (b_codes, b_scales)

        def multiply(t, operand, shared):
            b_codes, b_scales = operand
            res = work.tile([P, NO], F32, tag="res", bufs=4)
            for n in range(2):
                acc = psum.tile([P, 512], F32, tag="acc")
                for c in range(2):
                    nc.tensor.matmul_mx(
                        out=acc[:],
                        lhsT=b_codes[:, c * P : (c + 1) * P].bitcast(FP8X4),
                        lhsT_scale=b_scales[:, c * P : (c + 1) * P],
                        rhs=w_codes[:, c, n * 512 : (n + 1) * 512].bitcast(FP8X4),
                        rhs_scale=w_scales[:, c, n * 512 : (n + 1) * 512],
                        start=(c == 0),
                        stop=(c == 1),
                    )
                if shared and n == 1:
                    nc.vector.tensor_copy(out=res[:, n * 512 : (n + 1) * 512], in_=acc[:])
                else:
                    nc.scalar.copy(out=res[:, n * 512 : (n + 1) * 512], in_=acc[:])
            nc.sync.dma_start(out=out_v[t], in_=res[:])

        def pieces(php, chain):
            at = work.tile([P, 24, W2], BF16, tag="at%s" % chain)
            f0 = pieces_a(php[0], 0)
            f1 = pieces_a(php[0], 1)
            for q in range(4):
                pa = pieces_b(f0 if q < 2 else f1, q % 2)
                pieces_c(at, pa, q)
            return at

        ex = ctx.enter_context(tc.tile_pool(name="ex", bufs=1))
        hn = NP // 2
        cn = NP // 4

        def outer_logs(half):
            qq = ex.tile([P, 8, hn], F32, tag="qq")
            hv = hh[:, half * hn : (half + 1) * hn]
            nc.scalar.activation(out=qq[:, 0, :], in_=hv, func=ACT.Relu, scale=-c31, bias=c31 * 0.5)
            nc.scalar.activation(out=qq[:, 7, :], in_=hv, func=ACT.Relu, scale=c31, bias=c31 * 0.5)
            for m in range(1, 4):
                nc.scalar.activation(out=qq[:, m, :], in_=hv, func=ACT.Ln, scale=-c31, bias=c31 * (m + 0.5))
                nc.scalar.activation(out=qq[:, 7 - m, :], in_=hv, func=ACT.Ln, scale=c31, bias=c31 * (m + 0.5))
            nc.scalar.activation(out=qq[:, mirror_rows(0), :], in_=qq[:, mirror_rows(0), :], func=ACT.Ln, bias=1.0e-18)
            return qq

        def outer_scalar(qq, ch):
            qc = qq[:, :, (ch % 2) * cn : (ch % 2 + 1) * cn]
            nc.scalar.activation(out=qc, in_=qc, func=ACT.Exp, scale=31.0)
            nc.scalar.copy(out=xe[:, mirror_rows(0), ch * cn : (ch + 1) * cn], in_=qc[:, mirror_rows(0), :])

        def outer_vector(qq, ch):
            qc = qq[:, :, (ch % 2) * cn : (ch % 2 + 1) * cn]
            xec = xe[:, :, ch * cn : (ch + 1) * cn]
            ta = ex.tile([P, 2, cn], F32, tag="ta")
            tb3 = ex.tile([P, 2, cn], F32, tag="tb3")
            tc3 = ex.tile([P, 2, cn], F32, tag="tc3")
            nc.vector.scalar_tensor_tensor(out=ta[:], in0=qc[:, mirror_rows(1), :], scalar=-32.0, in1=qc[:, mirror_rows(2), :], op0=ALU.mult, op1=ALU.add)
            nc.vector.scalar_tensor_tensor(out=tb3[:], in0=qc[:, mirror_rows(2), :], scalar=-32.0, in1=qc[:, mirror_rows(3), :], op0=ALU.mult, op1=ALU.add)
            nc.vector.scalar_tensor_tensor(out=xec[:, mirror_rows(1), :], in0=qc[:, mirror_rows(0), :], scalar=-32.0, in1=qc[:, mirror_rows(1), :], op0=ALU.mult, op1=ALU.add)
            nc.vector.scalar_tensor_tensor(out=tc3[:], in0=qc[:, mirror_rows(1), :], scalar=496.0, in1=tb3[:], op0=ALU.mult, op1=ALU.add)
            nc.vector.scalar_tensor_tensor(out=xec[:, mirror_rows(2), :], in0=qc[:, mirror_rows(0), :], scalar=496.0, in1=ta[:], op0=ALU.mult, op1=ALU.add)
            nc.vector.scalar_tensor_tensor(out=xec[:, mirror_rows(3), :], in0=qc[:, mirror_rows(0), :], scalar=-4960.0, in1=tc3[:], op0=ALU.mult, op1=ALU.add)
            for first, mm in ((0, mu_pos[4]), (4, mu_neg[4])):
                nc.vector.tensor_tensor(
                    out=xec[:, first : first + 4, :],
                    in0=xec[:, first : first + 4, :],
                    in1=mm[:, ch * cn : (ch + 1) * cn].unsqueeze(1).to_broadcast([P, 4, cn]),
                    op=ALU.mult,
                )

        php_a = powers_start(0)
        php_b = powers_start(1)
        taylor_matrix()
        for lv in range(3):
            powers_step(php_a, lv)
            powers_step(php_b, lv)
        qq_cur = outer_logs(0)
        outer_scalar(qq_cur, 0)
        outer_vector(qq_cur, 0)
        at_a = pieces(php_a, "a")
        php_a = powers_start(2)
        for lv in range(3):
            powers_step(php_a, lv)
        at_b = pieces(php_b, "b")
        php_b = powers_start(3)

        fin_a = None
        fin_b = None
        for m in range(NQ):
            shifting = True
            finishing = m >= 1
            preparing = m + 1 < NQ
            ahead = m + 2 < NQ
            da = 2 * m
            db = 2 * m + 1
            t0 = 4 * (m - 1)
            old_a = at_a
            old_b = at_b
            if m == 0:
                outer_scalar(qq_cur, 1)
            if finishing:
                yc0 = turn_a(fin_a, 0)
            if preparing:
                at_a = work.tile([P, 24, W2], BF16, tag="ata")
                f0 = pieces_a(php_a[0], 0)
            if finishing:
                yc1 = turn_a(fin_a, 1)
                xt0 = turn_b(yc0)
            if preparing:
                p0 = pieces_b(f0, 0)
            if finishing:
                grouped0 = turn_c(xt0)
            if shifting:
                ya = first_pick("a", da, old_a)
                yb = first_pick("b", db, old_b)
            if preparing:
                powers_step(php_b, 0)
                pieces_c(at_a, p0, 0)
            if finishing:
                xt1 = turn_b(yc1)
            if preparing:
                p1 = pieces_b(f0, 1)
            if finishing:
                yc2 = turn_a(fin_b, 0)
            if preparing:
                f1 = pieces_a(php_a[0], 1)
            if finishing:
                grouped1 = turn_c(xt1)
            if preparing:
                pieces_c(at_a, p1, 1)
            if shifting:
                ga = shift_sign("a", da, 3, ya)
                gb = shift_sign("b", db, 3, yb)
            if preparing:
                powers_step(php_b, 1)
            if shifting:
                ya = shift_pick("a", 3, ga)
                yb = shift_pick("b", 3, gb)
            if preparing:
                powers_step(php_b, 2)
            if finishing:
                xt2 = turn_b(yc2)
            if preparing:
                p2 = pieces_b(f1, 0)
            if finishing:
                yc3 = turn_a(fin_b, 1)
                grouped2 = turn_c(xt2)
            if preparing:
                pieces_c(at_a, p2, 2)
            if finishing:
                xt3 = turn_b(yc3)
            if preparing:
                p3 = pieces_b(f1, 1)
            if finishing:
                grouped3 = turn_c(xt3)
            if preparing:
                pieces_c(at_a, p3, 3)
            if ahead:
                php_a = powers_start(da + 4)
            if shifting:
                ga = shift_sign("a", da, 2, ya)
                gb = shift_sign("b", db, 2, yb)
                ya = shift_pick("a", 2, ga)
                yb = shift_pick("b", 2, gb)
            if m == 1:
                quantise_weights()
            if finishing:
                op0 = quantise(grouped0)
            if preparing:
                at_b = work.tile([P, 24, W2], BF16, tag="atb")
                f0 = pieces_a(php_b[0], 0)
                f1 = pieces_a(php_b[0], 1)
                p0 = pieces_b(f0, 0)
            if finishing:
                multiply(t0, op0, False)
            if preparing:
                pieces_c(at_b, p0, 0)
                p1 = pieces_b(f0, 1)
                pieces_c(at_b, p1, 1)
            if shifting:
                ga = shift_sign("a", da, 1, ya)
                gb = shift_sign("b", db, 1, yb)
            if finishing:
                op1 = quantise(grouped1)
            if shifting:
                ya = shift_pick("a", 1, ga)
                yb = shift_pick("b", 1, gb)
            if finishing:
                op2 = quantise(grouped2)
                multiply(t0 + 1, op1, False)
            if preparing:
                p2 = pieces_b(f1, 0)
                pieces_c(at_b, p2, 2)
                p3 = pieces_b(f1, 1)
                pieces_c(at_b, p3, 3)
            if ahead:
                php_b = powers_start(db + 4)
            if finishing:
                multiply(t0 + 2, op2, False)
            if shifting:
                ga = shift_sign("a", da, 0, ya)
                gb = shift_sign("b", db, 0, yb)
            if finishing:
                op3 = quantise(grouped3)
            if shifting:
                ya = shift_pick("a", 0, ga)
                yb = shift_pick("b", 0, gb)
            if ahead:
                powers_step(php_a, 0)
            if finishing:
                multiply(t0 + 3, op3, False)
            if m == 0:
                outer_vector(qq_cur, 1)
                qq_cur = outer_logs(1)
                for a in range(4, 8):
                    weights_block(a)
            if m == 1 or m == 2:
                outer_scalar(qq_cur, m + 1)
            if shifting:
                ga = flip_sign("a", da, ya)
                gb = flip_sign("b", db, yb)
            if ahead:
                powers_step(php_a, 1)
            if shifting:
                fin_a = flip_pick("a", ga)
                fin_b = flip_pick("b", gb)
            if ahead:
                powers_step(php_a, 2)
            if m == 2 or m == 3:
                outer_vector(qq_cur, m)

        t0 = NT - 4
        yc0 = turn_a(fin_a, 0)
        yc2 = turn_a_vector(fin_b, 0)
        yc1 = turn_a(fin_a, 1)
        yc3 = turn_a_vector(fin_b, 1)
        xt2 = turn_b(yc2)
        xt0 = turn_b(yc0)
        op2 = quantise(turn_c_vector(xt2))
        xt3 = turn_b(yc3)
        multiply(t0 + 2, op2, False)
        op0 = quantise(turn_c_vector(xt0))
        xt1 = turn_b(yc1)
        op3 = quantise(turn_c_vector(xt3))
        multiply(t0, op0, False)
        op1 = quantise(turn_c_vector(xt1))
        multiply(t0 + 3, op3, True)
        multiply(t0 + 1, op1, True)
